import numpy as np
import ml_dtypes


def mxq(x, axis, fmt="e4m3"):
    dtype, down = {"e4m3": (ml_dtypes.float8_e4m3fn, 7), "e5m2": (ml_dtypes.float8_e5m2, 14)}[fmt]
    v = np.moveaxis(np.asarray(x, np.float32).astype(ml_dtypes.bfloat16).astype(np.float64), axis, -1)
    blocks = v.reshape(v.shape[:-1] + (-1, 32))
    amax = np.abs(blocks).max(-1, keepdims=True)
    byte = np.maximum(np.where(amax > 0, np.frexp(amax)[1] - 1 + 127, 0) - down, 1)
    scale = np.exp2(byte - 127.0)
    codes = (blocks / scale).astype(np.float32).astype(dtype).astype(np.float64)
    return np.moveaxis((codes * scale).reshape(v.shape), -1, axis)


WIDE = False


def mx_kscale(k):
    if not WIDE:
        return np.ones(k)
    levels = np.array([10, -10, 5, -5, 0])
    a = np.random.permutation(np.resize(levels, k // 512 * 4)).reshape(k // 512, 4)
    idx = np.arange(k)
    return np.exp2(a[idx // 512, idx % 128 // 32])


BF16 = ml_dtypes.bfloat16


def bf(x):
    return np.asarray(x, np.float32).astype(BF16)


def f64(x):
    return np.asarray(x).astype(np.float64)


B, D_IN, H, D_OUT, DEPTH, Q = 512, 1024, 2048, 1024, 3, 2


def quantum_probs(qw):
    n = qw.shape[1]
    s0r, s0i, s1r, s1i = np.ones(n), np.zeros(n), np.zeros(n), np.zeros(n)
    for d in range(qw.shape[0]):
        th = qw[d, :, 0, 0]
        ph = qw[d, :, 1, 1]
        c, s = np.cos(th), np.sin(th)
        n0r, n0i = c * s0r - s * s1r, c * s0i - s * s1i
        n1r, n1i = s * s0r + c * s1r, s * s0i + c * s1i
        cp, sp = np.cos(ph), np.sin(ph)
        s0r, s0i = n0r, n0i
        s1r, s1i = n1r * cp - n1i * sp, n1r * sp + n1i * cp
    return s0r * s0r + s0i * s0i


def setup_inputs():
    s, t = mx_kscale(H), mx_kscale(H)
    return {"h0": bf(np.maximum(np.random.standard_normal((B, H)), 0.0) * s),
            "w1": bf(np.random.standard_normal((H, H)) * 1.4 / np.sqrt(H) / s[:, None] * t),
            "b1": bf(np.random.standard_normal(H) * 0.3 * t),
            "q1_qw": bf(np.random.standard_normal((DEPTH, H, Q, Q))),
            "q1_cw": bf(np.random.standard_normal((H, H)) * 1.4 / np.sqrt(H) / t[:, None]),
            "q1_cb": bf(np.random.standard_normal(H) * 0.3)}


def reference(h0, w1, b1, q1_qw, q1_cw, q1_cb):
    h1 = np.maximum((mxq(f64(h0), 1, "e4m3") @ mxq(f64(w1), 0, "e4m3")) + f64(b1), 0.0)
    return np.tanh((mxq(h1, 1, "e4m3") @ mxq(f64(q1_cw), 0, "e4m3")) + f64(q1_cb) + quantum_probs(f64(q1_qw))[None, :])

@@ -1,0 +1,322 @@
+import math
+from contextlib import ExitStack
+
+import concourse.mybir as mybir
+from concourse.masks import make_identity
+
+F32 = mybir.dt.float32
+BF16 = mybir.dt.bfloat16
+U32 = mybir.dt.uint32
+U8 = mybir.dt.uint8
+FP8X4 = mybir.dt.float8_e4m3fn_x4
+ACT = mybir.ActivationFunctionType
+ALU = mybir.AluOpType
+
+P = 128
+PACK = 4
+K_PASS = P * PACK
+B = 512
+H = 2048
+DEPTH = 3
+PASSES = H // K_PASS
+B_TILES = B // P
+H_TILES = H // P
+SLICE = 512
+GROUPS = H // SLICE
+HALF = 1024
+SLICES = HALF // SLICE
+HALVES = H // HALF
+RUN = 4
+VECTOR_COLS_1 = 336
+VECTOR_COLS_2 = 248
+HALVES_IN_SBUF = 3
+
+ANGLES = DEPTH * H_TILES
+FILLED_ROWS = ANGLES + H_TILES
+ROUND_MAGIC = 1.5 * 2.0**23
+TWO_PI_HI = 6.28125
+TWO_PI_LO = 2.0 * math.pi - TWO_PI_HI
+PI_SAFE = 3.1415925
+
+FLOPS = 2 * (2 * B * H * H)
+
+
+def regroup(nc, grouped_pool, rows, vector_cols):
+    grouped = grouped_pool.tile([P, SLICE, PACK], BF16, align_bytes=64, tag="grouped")
+    vector_share = slice(0, vector_cols)
+    scalar_share = slice(vector_cols, SLICE)
+    nc.vector.tensor_copy(
+        out=grouped[:, vector_share, :].rearrange("p (c i) t -> p c t i", i=RUN),
+        in_=rows[:, :, vector_share].rearrange("p t (c i) -> p c t i", i=RUN),
+    )
+    nc.scalar.copy(
+        out=grouped[:, scalar_share, :].rearrange("p (c i) t -> p c t i", i=RUN),
+        in_=rows[:, :, scalar_share].rearrange("p t (c i) -> p c t i", i=RUN),
+    )
+    return grouped
+
+
+def quantise(nc, grouped, codes, scales):
+    nc.vector.quantize_mx(
+        out=codes.bitcast(FP8X4),
+        scales=scales,
+        in_=grouped[:].rearrange("p c t -> p (c t)"),
+    )
+
+
+def tile_quantumneuralnetwork_pa_kernel(tc, h0, w1, b1, q1_qw, q1_cw, q1_cb, out):
+    nc = tc.nc
+    with ExitStack() as ctx:
+        ctx.enter_context(tc.manual_schedule())
+        keep = ctx.enter_context(tc.tile_pool(name="keep", bufs=1))
+        raw_pool = ctx.enter_context(tc.tile_pool(name="raw", bufs=HALVES_IN_SBUF * PASSES))
+        grouped_pool = ctx.enter_context(tc.tile_pool(name="grouped", bufs=6))
+        weight_pool = ctx.enter_context(tc.tile_pool(name="weight", bufs=3))
+        h1_pool = ctx.enter_context(tc.tile_pool(name="h1", bufs=2))
+        out_pool = ctx.enter_context(tc.tile_pool(name="out", bufs=6))
+        psum = ctx.enter_context(tc.psum_pool(name="psum", bufs=8))
+
+        qw_rows = keep.tile([ANGLES, P, PACK], BF16)
+        small_rows = keep.tile([P, 2, P], BF16)
+        nc.sync.dma_start(out=qw_rows[:], in_=q1_qw.rearrange("d (m q) a b -> (d m) q (a b)", q=P))
+        nc.sync.dma_start(
+            out=small_rows[ANGLES:FILLED_ROWS, 0, :], in_=b1.rearrange("(m q) -> m q", q=P)
+        )
+        nc.sync.dma_start(
+            out=small_rows[ANGLES:FILLED_ROWS, 1, :], in_=q1_cb.rearrange("(m q) -> m q", q=P)
+        )
+        h0_sb = keep.tile([P, B_TILES, H], BF16)
+        for bt in range(B_TILES):
+            nc.sync.dma_start(out=h0_sb[:, bt, :], in_=h0[bt * P : (bt + 1) * P, :])
+
+        def chunk_view(half, c, cols):
+            if half < HALVES:
+                rows = w1[c * K_PASS : (c + 1) * K_PASS, half * HALF : (half + 1) * HALF]
+                return rows.rearrange("(p t) n -> p t n", t=PACK)[:, :, cols]
+            rows = q1_cw[c * K_PASS : (c + 1) * K_PASS, (half - HALVES) * HALF : (half - HALVES + 1) * HALF]
+            return rows.rearrange("(t p) n -> p t n", p=P)[:, :, cols]
+
+        halves = []
+
+        def load_half(pieces):
+            half = len(halves)
+            chunks = [
+                raw_pool.tile([P, PACK, HALF], BF16, tag="raw", name="raw%d" % c) for c in range(PASSES)
+            ]
+            for piece in range(pieces):
+                cols = slice(piece * (HALF // pieces), (piece + 1) * (HALF // pieces))
+                for c in range(PASSES):
+                    nc.sync.dma_start(out=chunks[c][:, :, cols], in_=chunk_view(half, c, cols))
+            halves.append(chunks)
+
+        load_half(SLICES)
+        for i in range(1, HALVES_IN_SBUF):
+            load_half(1)
+
+        ident_f32 = keep.tile([P, P], F32)
+        make_identity(nc, ident_f32[:])
+        ident_bf16 = keep.tile([P, P], BF16)
+        nc.vector.tensor_copy(out=ident_bf16[:], in_=ident_f32[:])
+
+        nc.vector.memset(small_rows[FILLED_ROWS:P], 0.0)
+        nc.vector.tensor_copy(
+            out=small_rows[0:ANGLES], in_=qw_rows[:].rearrange("r q e -> r e q")[:, 0:PACK:3, :]
+        )
+        small_cols = psum.tile([P, 2, P], BF16, tag="bank")
+        for h in range(2):
+            nc.tensor.transpose(small_cols[:, h, :], small_rows[:, h, :], ident_bf16[:])
+
+        args = keep.tile([P, 2, 2, ANGLES], F32)
+        nc.vector.tensor_copy(out=args[:, 0], in_=small_cols[:, :, 0:ANGLES])
+        nc.vector.tensor_scalar_add(
+            out=args[:, 1], in0=small_cols[:, :, 0:ANGLES], scalar1=math.pi / 2.0
+        )
+        args_flat = args[:].rearrange("p f h r -> p (f h r)")
+        turns = keep.tile([P, 2 * 2 * ANGLES], F32)
+        nc.vector.tensor_scalar(
+            out=turns[:], in0=args_flat, scalar1=1.0 / (2.0 * math.pi), scalar2=ROUND_MAGIC,
+            op0=ALU.mult, op1=ALU.add,
+        )
+        nc.vector.tensor_scalar_sub(out=turns[:], in0=turns[:], scalar1=ROUND_MAGIC)
+        for part in (TWO_PI_HI, TWO_PI_LO):
+            nc.vector.scalar_tensor_tensor(
+                out=args_flat, in0=turns[:], scalar=-part, in1=args_flat,
+                op0=ALU.mult, op1=ALU.add,
+            )
+        nc.vector.tensor_scalar(
+            out=args_flat, in0=args_flat, scalar1=-PI_SAFE, scalar2=PI_SAFE,
+            op0=ALU.max, op1=ALU.min,
+        )
+        sincos = keep.tile([P, 2, 2, DEPTH, H_TILES], F32)
+        nc.scalar.activation(
+            out=sincos[:].rearrange("p f h d m -> p (f h d m)"), in_=args_flat, func=ACT.Sin
+        )
+        biases = keep.tile([P, 2, H_TILES], F32)
+        nc.vector.tensor_copy(out=biases[:], in_=small_cols[:, :, ANGLES:FILLED_ROWS])
+
+        def spread(f, h, d, copies):
+            return sincos[:, f, h, d, :].unsqueeze(1).to_broadcast([P, copies, H_TILES])
+
+        amp = keep.tile([P, 2, 2, H_TILES], F32)
+        nc.vector.memset(amp[:], 0.0)
+        nc.vector.memset(amp[:, 0, 0, :], 1.0)
+        by_cos = keep.tile([P, 2, 2, H_TILES], F32)
+        by_sin = keep.tile([P, 2, 2, H_TILES], F32)
+        turned = keep.tile([P, 2, H_TILES], F32)
+        amp_parts = amp[:].rearrange("p a r m -> p (a r) m")
+        for d in range(DEPTH):
+            nc.vector.tensor_mul(
+                out=by_cos[:].rearrange("p a r m -> p (a r) m"), in0=amp_parts, in1=spread(1, 0, d, 4)
+            )
+            nc.vector.tensor_mul(
+                out=by_sin[:].rearrange("p a r m -> p (a r) m"), in0=amp_parts, in1=spread(0, 0, d, 4)
+            )
+            nc.vector.tensor_sub(out=amp[:, 0], in0=by_cos[:, 0], in1=by_sin[:, 1])
+            if d < DEPTH - 1:
+                nc.vector.tensor_add(out=turned[:], in0=by_sin[:, 0], in1=by_cos[:, 1])
+                nc.vector.tensor_mul(out=by_cos[:, 0], in0=turned[:], in1=spread(1, 1, d, 2))
+                nc.vector.tensor_mul(out=by_sin[:, 0], in0=turned[:], in1=spread(0, 1, d, 2))
+                nc.vector.tensor_sub(
+                    out=amp[:, 1, 0, :], in0=by_cos[:, 0, 0, :], in1=by_sin[:, 0, 1, :]
+                )
+                nc.vector.tensor_add(
+                    out=amp[:, 1, 1, :], in0=by_sin[:, 0, 0, :], in1=by_cos[:, 0, 1, :]
+                )
+        out_bias = keep.tile([P, H_TILES], F32)
+        nc.vector.tensor_mul(out=turned[:], in0=amp[:, 0], in1=amp[:, 0])
+        nc.vector.tensor_add(out=out_bias[:], in0=turned[:, 0, :], in1=turned[:, 1, :])
+        nc.vector.tensor_add(out=out_bias[:], in0=out_bias[:], in1=biases[:, 1, :])
+        out_bias_rows = keep.tile([P, H], F32)
+
+        def spread_out_bias(n):
+            bank = psum.tile([P, SLICE], F32, tag="bank")
+            for i in range(SLICE // P):
+                m = n * (SLICE // P) + i
+                nc.tensor.matmul(
+                    out=bank[:, i * P : (i + 1) * P],
+                    lhsT=out_bias[:, m : m + 1].to_broadcast([P, P]),
+                    rhs=ident_f32[:],
+                    start=True,
+                    stop=True,
+                )
+            nc.scalar.copy(out=out_bias_rows[:, n * SLICE : (n + 1) * SLICE], in_=bank[:])
+
+        h0_words = h0_sb[:].bitcast(F32)
+        words_in_pass = K_PASS // 2
+        h0_codes = keep.tile([P, PASSES, B], U32, align_bytes=64)
+        h0_scales = keep.tile([P, PASSES, B], U8, align_bytes=64)
+        h0_grouped = [
+            grouped_pool.tile([P, B, PACK], BF16, align_bytes=64, tag="grouped", name="h0_grouped%d" % c)
+            for c in range(PASSES)
+        ]
+        for pair in range(B_TILES // 2):
+            for c in range(PASSES):
+                bank = psum.tile([P, 2, 2, P], F32, tag="bank")
+                for u in range(2):
+                    for i in range(2):
+                        nc.tensor.transpose(
+                            bank[:, u, i, :],
+                            h0_words[:, 2 * pair + i, c * words_in_pass + u : (c + 1) * words_in_pass : 2],
+                            ident_f32[:],
+                        )
+                copy_out = nc.scalar.copy if pair == 0 else nc.vector.tensor_copy
+                copy_out(
+                    out=h0_grouped[c][:].bitcast(F32)[:, 2 * pair * P : 2 * (pair + 1) * P, :],
+                    in_=bank[:].rearrange("p u i b -> p (i b) u"),
+                )
+        for c in range(PASSES):
+            quantise(nc, h0_grouped[c], h0_codes[:, c, :], h0_scales[:, c, :])
+
+        h1_codes = keep.tile([P, PASSES, B], U32, align_bytes=64)
+        h1_scales = keep.tile([P, PASSES, B], U8, align_bytes=64)
+
+        def relu(h1_rows, g, t, bank):
+            m = g * PACK + t
+            nc.scalar.activation(
+                out=h1_rows[:, t, :], in_=bank[:], func=ACT.Relu, bias=biases[:, 0, m : m + 1]
+            )
+
+        def quantise_h1(h1_rows, g):
+            grouped = regroup(nc, grouped_pool, h1_rows[:], VECTOR_COLS_1)
+            quantise(nc, grouped, h1_codes[:, g, :], h1_scales[:, g, :])
+
+        def finish_out(n, bt, bank):
+            cols = slice(n * SLICE, (n + 1) * SLICE)
+            result = out_pool.tile([P, SLICE], F32, tag="result")
+            nc.vector.tensor_add(out=result[:], in0=bank[:], in1=out_bias_rows[:, cols])
+            nc.scalar.activation(out=result[:], in_=result[:], func=ACT.Tanh)
+            nc.sync.dma_start(out=out[bt * P : (bt + 1) * P, cols], in_=result[:])
+
+        banks = None
+        h1_rows = None
+        for g in range(GROUPS):
+            chunks = halves[g // SLICES]
+            cols = slice((g % SLICES) * SLICE, (g % SLICES + 1) * SLICE)
+            codes = weight_pool.tile([P, PASSES, SLICE], U32, align_bytes=64, tag="codes")
+            scales = weight_pool.tile([P, PASSES, SLICE], U8, align_bytes=64, tag="scales")
+            last_banks = banks
+            banks = [psum.tile([P, B], F32, tag="bank", name="h1_bank%d" % t) for t in range(PACK)]
+            if g > 0:
+                h1_rows = h1_pool.tile([P, PACK, B], BF16, tag="h1_rows")
+            for first in range(0, PASSES, 2):
+                pair = (first, first + 1)
+                grouped = [regroup(nc, grouped_pool, chunks[c][:, :, cols], VECTOR_COLS_1) for c in pair]
+                for i in pair:
+                    if g == 0:
+                        spread_out_bias(i)
+                    else:
+                        relu(h1_rows, g - 1, i, last_banks[i])
+                for c in pair:
+                    quantise(nc, grouped[c - first], codes[:, c, :], scales[:, c, :])
+                if g > 0 and first == PASSES - 2:
+                    quantise_h1(h1_rows, g - 1)
+                for t in range(PACK):
+                    units = slice(t * P, (t + 1) * P)
+                    for c in pair:
+                        nc.tensor.matmul_mx(
+                            out=banks[t][:],
+                            lhsT=codes[:, c, units].bitcast(FP8X4),
+                            lhsT_scale=scales[:, c, units],
+                            rhs=h0_codes[:, c, :].bitcast(FP8X4),
+                            rhs_scale=h0_scales[:, c, :],
+                            start=(c == 0),
+                            stop=(c == PASSES - 1),
+                        )
+            if g == SLICES - 1:
+                load_half(1)
+
+        for n in range(GROUPS):
+            chunks = halves[HALVES + n // SLICES]
+            cols = slice((n % SLICES) * SLICE, (n % SLICES + 1) * SLICE)
+            codes = weight_pool.tile([P, PASSES, SLICE], U32, align_bytes=64, tag="codes")
+            scales = weight_pool.tile([P, PASSES, SLICE], U8, align_bytes=64, tag="scales")
+            last_banks = banks
+            banks = [psum.tile([P, SLICE], F32, tag="bank", name="out_bank%d" % bt) for bt in range(B_TILES)]
+            if n == 0:
+                h1_rows = h1_pool.tile([P, PACK, B], BF16, tag="h1_rows")
+            for first in range(0, PASSES, 2):
+                pair = (first, first + 1)
+                grouped = [regroup(nc, grouped_pool, chunks[g][:, :, cols], VECTOR_COLS_2) for g in pair]
+                for i in pair:
+                    if n == 0:
+                        relu(h1_rows, GROUPS - 1, i, last_banks[i])
+                    else:
+                        finish_out(n - 1, i, last_banks[i])
+                for g in pair:
+                    quantise(nc, grouped[g - first], codes[:, g, :], scales[:, g, :])
+                if n == 0 and first == PASSES - 2:
+                    quantise_h1(h1_rows, GROUPS - 1)
+                for bt in range(B_TILES):
+                    rows = slice(bt * P, (bt + 1) * P)
+                    for g in pair:
+                        nc.tensor.matmul_mx(
+                            out=banks[bt][:],
+                            lhsT=h1_codes[:, g, rows].bitcast(FP8X4),
+                            lhsT_scale=h1_scales[:, g, rows],
+                            rhs=codes[:, g, :].bitcast(FP8X4),
+                            rhs_scale=scales[:, g, :],
+                            start=(g == 0),
+                            stop=(g == PASSES - 1),
+                        )
+        for bt in range(B_TILES):
+            finish_out(GROUPS - 1, bt, banks[bt])

@@ -41,8 +41,7 @@ PI_SAFE = 3.1415925
 FLOPS = 2 * (2 * B * H * H)
 
 
-def regroup(nc, grouped_pool, rows, vector_cols):
-    grouped = grouped_pool.tile([P, SLICE, PACK], BF16, align_bytes=64, tag="grouped")
+def regroup(nc, rows, grouped, vector_cols):
     vector_share = slice(0, vector_cols)
     scalar_share = slice(vector_cols, SLICE)
     nc.vector.tensor_copy(
@@ -53,15 +52,10 @@ def regroup(nc, grouped_pool, rows, vector_cols):
         out=grouped[:, scalar_share, :].rearrange("p (c i) t -> p c t i", i=RUN),
         in_=rows[:, :, scalar_share].rearrange("p t (c i) -> p c t i", i=RUN),
     )
-    return grouped
 
 
 def quantise(nc, grouped, codes, scales):
-    nc.vector.quantize_mx(
-        out=codes.bitcast(FP8X4),
-        scales=scales,
-        in_=grouped[:].rearrange("p c t -> p (c t)"),
-    )
+    nc.vector.quantize_mx(out=codes.bitcast(FP8X4), scales=scales, in_=grouped)
 
 
 def tile_quantumneuralnetwork_pa_kernel(tc, h0, w1, b1, q1_qw, q1_cw, q1_cb, out):
@@ -70,7 +64,7 @@ def tile_quantumneuralnetwork_pa_kernel(tc, h0, w1, b1, q1_qw, q1_cw, q1_cb, out
         ctx.enter_context(tc.manual_schedule())
         keep = ctx.enter_context(tc.tile_pool(name="keep", bufs=1))
         raw_pool = ctx.enter_context(tc.tile_pool(name="raw", bufs=HALVES_IN_SBUF * PASSES))
-        grouped_pool = ctx.enter_context(tc.tile_pool(name="grouped", bufs=6))
+        grouped_pool = ctx.enter_context(tc.tile_pool(name="grouped", bufs=3))
         weight_pool = ctx.enter_context(tc.tile_pool(name="weight", bufs=3))
         h1_pool = ctx.enter_context(tc.tile_pool(name="h1", bufs=2))
         out_pool = ctx.enter_context(tc.tile_pool(name="out", bufs=6))
@@ -151,6 +145,8 @@ def tile_quantumneuralnetwork_pa_kernel(tc, h0, w1, b1, q1_qw, q1_cw, q1_cb, out
         nc.scalar.activation(
             out=sincos[:].rearrange("p f h d m -> p (f h d m)"), in_=args_flat, func=ACT.Sin
         )
+        warm = keep.tile([P, 1], F32)
+        nc.scalar.activation(out=warm[:], in_=sincos[:, 0, 0, 0, 0:1], func=ACT.Tanh)
         biases = keep.tile([P, 2, H_TILES], F32)
         nc.vector.tensor_copy(out=biases[:], in_=small_cols[:, :, ANGLES:FILLED_ROWS])
 
@@ -186,10 +182,18 @@ def tile_quantumneuralnetwork_pa_kernel(tc, h0, w1, b1, q1_qw, q1_cw, q1_cb, out
         nc.vector.tensor_mul(out=turned[:], in0=amp[:, 0], in1=amp[:, 0])
         nc.vector.tensor_add(out=out_bias[:], in0=turned[:, 0, :], in1=turned[:, 1, :])
         nc.vector.tensor_add(out=out_bias[:], in0=out_bias[:], in1=biases[:, 1, :])
+        def quantise_pair(grouped, codes, scales, first):
+            quantise(
+                nc,
+                grouped[:].rearrange("p j c t -> p (j c t)"),
+                codes[:, first : first + 2, :].rearrange("p j c -> p (j c)"),
+                scales[:, first : first + 2, :].rearrange("p j c -> p (j c)"),
+            )
+
         out_bias_rows = keep.tile([P, H], F32)
 
         def spread_out_bias(n):
-            bank = psum.tile([P, SLICE], F32, tag="bank")
+            bank = psum.tile([P, SLICE], F32, tag="bank", name="bias_bank%d" % n)
             for i in range(SLICE // P):
                 m = n * (SLICE // P) + i
                 nc.tensor.matmul(
@@ -199,15 +203,15 @@ def tile_quantumneuralnetwork_pa_kernel(tc, h0, w1, b1, q1_qw, q1_cw, q1_cb, out
                     start=True,
                     stop=True,
                 )
-            nc.scalar.copy(out=out_bias_rows[:, n * SLICE : (n + 1) * SLICE], in_=bank[:])
+            return bank
 
         h0_words = h0_sb[:].bitcast(F32)
         words_in_pass = K_PASS // 2
         h0_codes = keep.tile([P, PASSES, B], U32, align_bytes=64)
         h0_scales = keep.tile([P, PASSES, B], U8, align_bytes=64)
         h0_grouped = [
-            grouped_pool.tile([P, B, PACK], BF16, align_bytes=64, tag="grouped", name="h0_grouped%d" % c)
-            for c in range(PASSES)
+            grouped_pool.tile([P, 2, B, PACK], BF16, align_bytes=64, tag="grouped", name="h0_grouped%d" % i)
+            for i in range(PASSES // 2)
         ]
         for pair in range(B_TILES // 2):
             for c in range(PASSES):
@@ -219,13 +223,13 @@ def tile_quantumneuralnetwork_pa_kernel(tc, h0, w1, b1, q1_qw, q1_cw, q1_cb, out
                             h0_words[:, 2 * pair + i, c * words_in_pass + u : (c + 1) * words_in_pass : 2],
                             ident_f32[:],
                         )
-                copy_out = nc.scalar.copy if pair == 0 else nc.vector.tensor_copy
-                copy_out(
-                    out=h0_grouped[c][:].bitcast(F32)[:, 2 * pair * P : 2 * (pair + 1) * P, :],
+                nc.scalar.copy(
+                    out=h0_grouped[c // 2][:, c % 2].bitcast(F32)[:, 2 * pair * P : 2 * (pair + 1) * P, :],
                     in_=bank[:].rearrange("p u i b -> p (i b) u"),
                 )
-        for c in range(PASSES):
-            quantise(nc, h0_grouped[c], h0_codes[:, c, :], h0_scales[:, c, :])
+        bias_banks = [spread_out_bias(n) for n in range(GROUPS)]
+        for first in range(0, PASSES, 2):
+            quantise_pair(h0_grouped[first // 2], h0_codes, h0_scales, first)
 
         h1_codes = keep.tile([P, PASSES, B], U32, align_bytes=64)
         h1_scales = keep.tile([P, PASSES, B], U8, align_bytes=64)
@@ -237,8 +241,9 @@ def tile_quantumneuralnetwork_pa_kernel(tc, h0, w1, b1, q1_qw, q1_cw, q1_cb, out
             )
 
         def quantise_h1(h1_rows, g):
-            grouped = regroup(nc, grouped_pool, h1_rows[:], VECTOR_COLS_1)
-            quantise(nc, grouped, h1_codes[:, g, :], h1_scales[:, g, :])
+            grouped = h1_pool.tile([P, B, PACK], BF16, align_bytes=64, tag="h1_grouped")
+            regroup(nc, h1_rows[:], grouped[:], VECTOR_COLS_1)
+            quantise(nc, grouped[:].rearrange("p b t -> p (b t)"), h1_codes[:, g, :], h1_scales[:, g, :])
 
         def finish_out(n, bt, bank):
             cols = slice(n * SLICE, (n + 1) * SLICE)
@@ -247,11 +252,26 @@ def tile_quantumneuralnetwork_pa_kernel(tc, h0, w1, b1, q1_qw, q1_cw, q1_cb, out
             nc.scalar.activation(out=result[:], in_=result[:], func=ACT.Tanh)
             nc.sync.dma_start(out=out[bt * P : (bt + 1) * P, cols], in_=result[:])
 
+        def regroup_pair(step):
+            group = step // 2
+            first = 2 * (step % 2)
+            chunks = halves[group // SLICES]
+            cols = slice((group % SLICES) * SLICE, (group % SLICES + 1) * SLICE)
+            grouped = grouped_pool.tile([P, 2, SLICE, PACK], BF16, align_bytes=64, tag="grouped")
+            for j in range(2):
+                regroup(
+                    nc,
+                    chunks[first + j][:, :, cols],
+                    grouped[:, j],
+                    VECTOR_COLS_1 if group < GROUPS else VECTOR_COLS_2,
+                )
+            return grouped
+
+        ahead = regroup_pair(0)
+
         banks = None
         h1_rows = None
         for g in range(GROUPS):
-            chunks = halves[g // SLICES]
-            cols = slice((g % SLICES) * SLICE, (g % SLICES + 1) * SLICE)
             codes = weight_pool.tile([P, PASSES, SLICE], U32, align_bytes=64, tag="codes")
             scales = weight_pool.tile([P, PASSES, SLICE], U8, align_bytes=64, tag="scales")
             last_banks = banks
@@ -260,14 +280,16 @@ def tile_quantumneuralnetwork_pa_kernel(tc, h0, w1, b1, q1_qw, q1_cw, q1_cb, out
                 h1_rows = h1_pool.tile([P, PACK, B], BF16, tag="h1_rows")
             for first in range(0, PASSES, 2):
                 pair = (first, first + 1)
-                grouped = [regroup(nc, grouped_pool, chunks[c][:, :, cols], VECTOR_COLS_1) for c in pair]
+                grouped = ahead
+                ahead = regroup_pair(2 * g + first // 2 + 1)
                 for i in pair:
                     if g == 0:
-                        spread_out_bias(i)
+                        nc.scalar.copy(
+                            out=out_bias_rows[:, i * SLICE : (i + 1) * SLICE], in_=bias_banks[i][:]
+                        )
                     else:
                         relu(h1_rows, g - 1, i, last_banks[i])
-                for c in pair:
-                    quantise(nc, grouped[c - first], codes[:, c, :], scales[:, c, :])
+                quantise_pair(grouped, codes, scales, first)
                 if g > 0 and first == PASSES - 2:
                     quantise_h1(h1_rows, g - 1)
                 for t in range(PACK):
@@ -286,8 +308,6 @@ def tile_quantumneuralnetwork_pa_kernel(tc, h0, w1, b1, q1_qw, q1_cw, q1_cb, out
                 load_half(1)
 
         for n in range(GROUPS):
-            chunks = halves[HALVES + n // SLICES]
-            cols = slice((n % SLICES) * SLICE, (n % SLICES + 1) * SLICE)
             codes = weight_pool.tile([P, PASSES, SLICE], U32, align_bytes=64, tag="codes")
             scales = weight_pool.tile([P, PASSES, SLICE], U8, align_bytes=64, tag="scales")
             last_banks = banks
@@ -296,14 +316,15 @@ def tile_quantumneuralnetwork_pa_kernel(tc, h0, w1, b1, q1_qw, q1_cw, q1_cb, out
                 h1_rows = h1_pool.tile([P, PACK, B], BF16, tag="h1_rows")
             for first in range(0, PASSES, 2):
                 pair = (first, first + 1)
-                grouped = [regroup(nc, grouped_pool, chunks[g][:, :, cols], VECTOR_COLS_2) for g in pair]
+                grouped = ahead
+                if n < GROUPS - 1 or first < PASSES - 2:
+                    ahead = regroup_pair(2 * (GROUPS + n) + first // 2 + 1)
                 for i in pair:
                     if n == 0:
                         relu(h1_rows, GROUPS - 1, i, last_banks[i])
                     else:
                         finish_out(n - 1, i, last_banks[i])
-                for g in pair:
-                    quantise(nc, grouped[g - first], codes[:, g, :], scales[:, g, :])
+                quantise_pair(grouped, codes, scales, first)
                 if n == 0 and first == PASSES - 2:
                     quantise_h1(h1_rows, GROUPS - 1)
                 for bt in range(B_TILES):

@@ -18,6 +18,8 @@ K_PASS = P * PACK
 B = 512
 H = 2048
 DEPTH = 3
+SIN, COS = 0, 1
+THETA, PHI = 0, 1
 PASSES = H // K_PASS
 B_TILES = B // P
 H_TILES = H // P
@@ -34,24 +36,26 @@ HALVES_IN_SBUF = 3
 ANGLES = DEPTH * H_TILES
 FILLED_ROWS = ANGLES + H_TILES
 ROUND_MAGIC = 1.5 * 2.0**23
-TWO_PI_HI = 6.28125
-TWO_PI_LO = 2.0 * math.pi - TWO_PI_HI
 PI_SAFE = 3.1415925
 
 FLOPS = 2 * (2 * B * H * H)
+
+
+def by_runs(rows):
+    return rows.rearrange("p t (c i) -> p c t i", i=RUN)
+
+
+def by_words(grouped):
+    return grouped.rearrange("p (c i) t -> p c t i", i=RUN)
 
 
 def regroup(nc, rows, grouped, vector_cols):
     vector_share = slice(0, vector_cols)
     scalar_share = slice(vector_cols, SLICE)
     nc.vector.tensor_copy(
-        out=grouped[:, vector_share, :].rearrange("p (c i) t -> p c t i", i=RUN),
-        in_=rows[:, :, vector_share].rearrange("p t (c i) -> p c t i", i=RUN),
+        out=by_words(grouped[:, vector_share, :]), in_=by_runs(rows[:, :, vector_share])
     )
-    nc.scalar.copy(
-        out=grouped[:, scalar_share, :].rearrange("p (c i) t -> p c t i", i=RUN),
-        in_=rows[:, :, scalar_share].rearrange("p t (c i) -> p c t i", i=RUN),
-    )
+    nc.scalar.copy(out=by_words(grouped[:, scalar_share, :]), in_=by_runs(rows[:, :, scalar_share]))
 
 
 def quantise(nc, grouped, codes, scales):
@@ -112,6 +116,12 @@ def tile_quantumneuralnetwork_pa_kernel(tc, h0, w1, b1, q1_qw, q1_cw, q1_cb, out
         ident_bf16 = keep.tile([P, P], BF16)
         nc.vector.tensor_copy(out=ident_bf16[:], in_=ident_f32[:])
 
+        angle_factor = keep.tile([P, 2, 1], F32)
+        nc.vector.memset(angle_factor[:, 0, :], 2.0)
+        nc.vector.memset(angle_factor[:, 1, :], 1.0)
+        warm = keep.tile([P, 1], F32)
+        nc.scalar.activation(out=warm[:], in_=angle_factor[:, 1, :], func=ACT.Sin)
+
         nc.vector.memset(small_rows[FILLED_ROWS:P], 0.0)
         nc.vector.tensor_copy(
             out=small_rows[0:ANGLES], in_=qw_rows[:].rearrange("r q e -> r e q")[:, 0:PACK:3, :]
@@ -121,10 +131,12 @@ def tile_quantumneuralnetwork_pa_kernel(tc, h0, w1, b1, q1_qw, q1_cw, q1_cb, out
             nc.tensor.transpose(small_cols[:, h, :], small_rows[:, h, :], ident_bf16[:])
 
         args = keep.tile([P, 2, 2, ANGLES], F32)
-        nc.vector.tensor_copy(out=args[:, 0], in_=small_cols[:, :, 0:ANGLES])
-        nc.vector.tensor_scalar_add(
-            out=args[:, 1], in0=small_cols[:, :, 0:ANGLES], scalar1=math.pi / 2.0
+        nc.vector.tensor_mul(
+            out=args[:, 0],
+            in0=small_cols[:, :, 0:ANGLES],
+            in1=angle_factor[:].to_broadcast([P, 2, ANGLES]),
         )
+        nc.vector.tensor_scalar_add(out=args[:, 1], in0=args[:, 0], scalar1=math.pi / 2.0)
         args_flat = args[:].rearrange("p f h r -> p (f h r)")
         turns = keep.tile([P, 2 * 2 * ANGLES], F32)
         nc.vector.tensor_scalar(
@@ -132,11 +144,10 @@ def tile_quantumneuralnetwork_pa_kernel(tc, h0, w1, b1, q1_qw, q1_cw, q1_cb, out
             op0=ALU.mult, op1=ALU.add,
         )
         nc.vector.tensor_scalar_sub(out=turns[:], in0=turns[:], scalar1=ROUND_MAGIC)
-        for part in (TWO_PI_HI, TWO_PI_LO):
-            nc.vector.scalar_tensor_tensor(
-                out=args_flat, in0=turns[:], scalar=-part, in1=args_flat,
-                op0=ALU.mult, op1=ALU.add,
-            )
+        nc.vector.scalar_tensor_tensor(
+            out=args_flat, in0=turns[:], scalar=-2.0 * math.pi, in1=args_flat,
+            op0=ALU.mult, op1=ALU.add,
+        )
         nc.vector.tensor_scalar(
             out=args_flat, in0=args_flat, scalar1=-PI_SAFE, scalar2=PI_SAFE,
             op0=ALU.max, op1=ALU.min,
@@ -145,43 +156,37 @@ def tile_quantumneuralnetwork_pa_kernel(tc, h0, w1, b1, q1_qw, q1_cw, q1_cb, out
         nc.scalar.activation(
             out=sincos[:].rearrange("p f h d m -> p (f h d m)"), in_=args_flat, func=ACT.Sin
         )
-        warm = keep.tile([P, 1], F32)
-        nc.scalar.activation(out=warm[:], in_=sincos[:, 0, 0, 0, 0:1], func=ACT.Tanh)
+        nc.scalar.activation(out=warm[:], in_=angle_factor[:, 1, :], func=ACT.Tanh)
         biases = keep.tile([P, 2, H_TILES], F32)
         nc.vector.tensor_copy(out=biases[:], in_=small_cols[:, :, ANGLES:FILLED_ROWS])
 
-        def spread(f, h, d, copies):
-            return sincos[:, f, h, d, :].unsqueeze(1).to_broadcast([P, copies, H_TILES])
+        def twice(table):
+            return table.unsqueeze(1).to_broadcast([P, 2, H_TILES])
 
-        amp = keep.tile([P, 2, 2, H_TILES], F32)
-        nc.vector.memset(amp[:], 0.0)
-        nc.vector.memset(amp[:, 0, 0, :], 1.0)
-        by_cos = keep.tile([P, 2, 2, H_TILES], F32)
-        by_sin = keep.tile([P, 2, 2, H_TILES], F32)
-        turned = keep.tile([P, 2, H_TILES], F32)
-        amp_parts = amp[:].rearrange("p a r m -> p (a r) m")
-        for d in range(DEPTH):
-            nc.vector.tensor_mul(
-                out=by_cos[:].rearrange("p a r m -> p (a r) m"), in0=amp_parts, in1=spread(1, 0, d, 4)
-            )
-            nc.vector.tensor_mul(
-                out=by_sin[:].rearrange("p a r m -> p (a r) m"), in0=amp_parts, in1=spread(0, 0, d, 4)
-            )
-            nc.vector.tensor_sub(out=amp[:, 0], in0=by_cos[:, 0], in1=by_sin[:, 1])
-            if d < DEPTH - 1:
-                nc.vector.tensor_add(out=turned[:], in0=by_sin[:, 0], in1=by_cos[:, 1])
-                nc.vector.tensor_mul(out=by_cos[:, 0], in0=turned[:], in1=spread(1, 1, d, 2))
-                nc.vector.tensor_mul(out=by_sin[:, 0], in0=turned[:], in1=spread(0, 1, d, 2))
-                nc.vector.tensor_sub(
-                    out=amp[:, 1, 0, :], in0=by_cos[:, 0, 0, :], in1=by_sin[:, 0, 1, :]
-                )
-                nc.vector.tensor_add(
-                    out=amp[:, 1, 1, :], in0=by_sin[:, 0, 0, :], in1=by_cos[:, 0, 1, :]
-                )
+        z0 = sincos[:, COS, THETA, 0, :]
+        yx0 = keep.tile([P, 2, H_TILES], F32)
+        nc.vector.tensor_mul(out=yx0[:], in0=sincos[:, :, PHI, 0, :], in1=twice(sincos[:, SIN, THETA, 0, :]))
+        by_z0 = keep.tile([P, 2, H_TILES], F32)
+        by_x0 = keep.tile([P, 2, H_TILES], F32)
+        nc.vector.tensor_mul(out=by_z0[:], in0=sincos[:, :, THETA, 1, :], in1=twice(z0))
+        nc.vector.tensor_mul(out=by_x0[:], in0=sincos[:, :, THETA, 1, :], in1=twice(yx0[:, 1, :]))
+        y_part = keep.tile([P, H_TILES], F32)
+        nc.vector.tensor_mul(out=y_part[:], in0=yx0[:, 0, :], in1=sincos[:, SIN, PHI, 1, :])
+        xz1 = keep.tile([P, 2, H_TILES], F32)
+        nc.vector.tensor_sub(out=xz1[:, 1, :], in0=by_z0[:, COS, :], in1=by_x0[:, SIN, :])
+        x_part = keep.tile([P, H_TILES], F32)
+        nc.vector.tensor_add(out=x_part[:], in0=by_z0[:, SIN, :], in1=by_x0[:, COS, :])
+        nc.vector.tensor_mul(out=x_part[:], in0=x_part[:], in1=sincos[:, COS, PHI, 1, :])
+        nc.vector.tensor_sub(out=xz1[:, 0, :], in0=x_part[:], in1=y_part[:])
+        by_xz1 = keep.tile([P, 2, H_TILES], F32)
+        nc.vector.tensor_mul(out=by_xz1[:], in0=sincos[:, :, THETA, 2, :], in1=xz1[:])
         out_bias = keep.tile([P, H_TILES], F32)
-        nc.vector.tensor_mul(out=turned[:], in0=amp[:, 0], in1=amp[:, 0])
-        nc.vector.tensor_add(out=out_bias[:], in0=turned[:, 0, :], in1=turned[:, 1, :])
+        nc.vector.tensor_sub(out=out_bias[:], in0=by_xz1[:, COS, :], in1=by_xz1[:, SIN, :])
+        nc.vector.tensor_scalar(
+            out=out_bias[:], in0=out_bias[:], scalar1=1.0, scalar2=0.5, op0=ALU.add, op1=ALU.mult
+        )
         nc.vector.tensor_add(out=out_bias[:], in0=out_bias[:], in1=biases[:, 1, :])
+
         def quantise_pair(grouped, codes, scales, first):
             quantise(
                 nc,
@@ -205,6 +210,21 @@ def tile_quantumneuralnetwork_pa_kernel(tc, h0, w1, b1, q1_qw, q1_cw, q1_cb, out
                 )
             return bank
 
+        def regroup_pair(step):
+            group = step // 2
+            first = 2 * (step % 2)
+            chunks = halves[group // SLICES]
+            cols = slice((group % SLICES) * SLICE, (group % SLICES + 1) * SLICE)
+            grouped = grouped_pool.tile([P, 2, SLICE, PACK], BF16, align_bytes=64, tag="grouped")
+            for j in range(2):
+                regroup(
+                    nc,
+                    chunks[first + j][:, :, cols],
+                    grouped[:, j],
+                    VECTOR_COLS_1 if group < GROUPS else VECTOR_COLS_2,
+                )
+            return grouped
+
         h0_words = h0_sb[:].bitcast(F32)
         words_in_pass = K_PASS // 2
         h0_codes = keep.tile([P, PASSES, B], U32, align_bytes=64)
@@ -227,7 +247,8 @@ def tile_quantumneuralnetwork_pa_kernel(tc, h0, w1, b1, q1_qw, q1_cw, q1_cb, out
                     out=h0_grouped[c // 2][:, c % 2].bitcast(F32)[:, 2 * pair * P : 2 * (pair + 1) * P, :],
                     in_=bank[:].rearrange("p u i b -> p (i b) u"),
                 )
-        bias_banks = [spread_out_bias(n) for n in range(GROUPS)]
+            if pair == 0:
+                ahead = regroup_pair(0)
         for first in range(0, PASSES, 2):
             quantise_pair(h0_grouped[first // 2], h0_codes, h0_scales, first)
 
@@ -242,8 +263,14 @@ def tile_quantumneuralnetwork_pa_kernel(tc, h0, w1, b1, q1_qw, q1_cw, q1_cb, out
 
         def quantise_h1(h1_rows, g):
             grouped = h1_pool.tile([P, B, PACK], BF16, align_bytes=64, tag="h1_grouped")
-            regroup(nc, h1_rows[:], grouped[:], VECTOR_COLS_1)
+            nc.vector.tensor_copy(out=by_words(grouped[:]), in_=by_runs(h1_rows[:]))
             quantise(nc, grouped[:].rearrange("p b t -> p (b t)"), h1_codes[:, g, :], h1_scales[:, g, :])
+
+        def bias_rows_step(n, first, bank):
+            if first == 0:
+                return spread_out_bias(n)
+            nc.scalar.copy(out=out_bias_rows[:, n * SLICE : (n + 1) * SLICE], in_=bank[:])
+            return None
 
         def finish_out(n, bt, bank):
             cols = slice(n * SLICE, (n + 1) * SLICE)
@@ -252,25 +279,9 @@ def tile_quantumneuralnetwork_pa_kernel(tc, h0, w1, b1, q1_qw, q1_cw, q1_cb, out
             nc.scalar.activation(out=result[:], in_=result[:], func=ACT.Tanh)
             nc.sync.dma_start(out=out[bt * P : (bt + 1) * P, cols], in_=result[:])
 
-        def regroup_pair(step):
-            group = step // 2
-            first = 2 * (step % 2)
-            chunks = halves[group // SLICES]
-            cols = slice((group % SLICES) * SLICE, (group % SLICES + 1) * SLICE)
-            grouped = grouped_pool.tile([P, 2, SLICE, PACK], BF16, align_bytes=64, tag="grouped")
-            for j in range(2):
-                regroup(
-                    nc,
-                    chunks[first + j][:, :, cols],
-                    grouped[:, j],
-                    VECTOR_COLS_1 if group < GROUPS else VECTOR_COLS_2,
-                )
-            return grouped
-
-        ahead = regroup_pair(0)
-
         banks = None
         h1_rows = None
+        bias_bank = None
         for g in range(GROUPS):
             codes = weight_pool.tile([P, PASSES, SLICE], U32, align_bytes=64, tag="codes")
             scales = weight_pool.tile([P, PASSES, SLICE], U8, align_bytes=64, tag="scales")
@@ -282,13 +293,10 @@ def tile_quantumneuralnetwork_pa_kernel(tc, h0, w1, b1, q1_qw, q1_cw, q1_cb, out
                 pair = (first, first + 1)
                 grouped = ahead
                 ahead = regroup_pair(2 * g + first // 2 + 1)
-                for i in pair:
-                    if g == 0:
-                        nc.scalar.copy(
-                            out=out_bias_rows[:, i * SLICE : (i + 1) * SLICE], in_=bias_banks[i][:]
-                        )
-                    else:
+                if g > 0:
+                    for i in pair:
                         relu(h1_rows, g - 1, i, last_banks[i])
+                    bias_bank = bias_rows_step(g - 1, first, bias_bank)
                 quantise_pair(grouped, codes, scales, first)
                 if g > 0 and first == PASSES - 2:
                     quantise_h1(h1_rows, g - 1)
@@ -324,6 +332,8 @@ def tile_quantumneuralnetwork_pa_kernel(tc, h0, w1, b1, q1_qw, q1_cw, q1_cb, out
                         relu(h1_rows, GROUPS - 1, i, last_banks[i])
                     else:
                         finish_out(n - 1, i, last_banks[i])
+                if n == 0:
+                    bias_bank = bias_rows_step(GROUPS - 1, first, bias_bank)
                 quantise_pair(grouped, codes, scales, first)
                 if n == 0 and first == PASSES - 2:
                     quantise_h1(h1_rows, GROUPS - 1)

@@ -55,7 +55,8 @@ def regroup(nc, rows, grouped, vector_cols):
     nc.vector.tensor_copy(
         out=by_words(grouped[:, vector_share, :]), in_=by_runs(rows[:, :, vector_share])
     )
-    nc.scalar.copy(out=by_words(grouped[:, scalar_share, :]), in_=by_runs(rows[:, :, scalar_share]))
+    if vector_cols < SLICE:
+        nc.scalar.copy(out=by_words(grouped[:, scalar_share, :]), in_=by_runs(rows[:, :, scalar_share]))
 
 
 def quantise(nc, grouped, codes, scales):
@@ -68,10 +69,10 @@ def tile_quantumneuralnetwork_pa_kernel(tc, h0, w1, b1, q1_qw, q1_cw, q1_cb, out
         ctx.enter_context(tc.manual_schedule())
         keep = ctx.enter_context(tc.tile_pool(name="keep", bufs=1))
         raw_pool = ctx.enter_context(tc.tile_pool(name="raw", bufs=HALVES_IN_SBUF * PASSES))
-        grouped_pool = ctx.enter_context(tc.tile_pool(name="grouped", bufs=3))
+        grouped_pool = ctx.enter_context(tc.tile_pool(name="grouped", bufs=4))
         weight_pool = ctx.enter_context(tc.tile_pool(name="weight", bufs=3))
         h1_pool = ctx.enter_context(tc.tile_pool(name="h1", bufs=2))
-        out_pool = ctx.enter_context(tc.tile_pool(name="out", bufs=6))
+        out_pool = ctx.enter_context(tc.tile_pool(name="out", bufs=4))
         psum = ctx.enter_context(tc.psum_pool(name="psum", bufs=8))
 
         qw_rows = keep.tile([ANGLES, P, PACK], BF16)
@@ -84,7 +85,8 @@ def tile_quantumneuralnetwork_pa_kernel(tc, h0, w1, b1, q1_qw, q1_cw, q1_cb, out
             out=small_rows[ANGLES:FILLED_ROWS, 1, :], in_=q1_cb.rearrange("(m q) -> m q", q=P)
         )
         h0_sb = keep.tile([P, B_TILES, H], BF16)
-        for bt in range(B_TILES):
+
+        def load_h0(bt):
             nc.sync.dma_start(out=h0_sb[:, bt, :], in_=h0[bt * P : (bt + 1) * P, :])
 
         def chunk_view(half, c, cols):
@@ -96,20 +98,33 @@ def tile_quantumneuralnetwork_pa_kernel(tc, h0, w1, b1, q1_qw, q1_cw, q1_cb, out
 
         halves = []
 
-        def load_half(pieces):
-            half = len(halves)
-            chunks = [
-                raw_pool.tile([P, PACK, HALF], BF16, tag="raw", name="raw%d" % c) for c in range(PASSES)
-            ]
-            for piece in range(pieces):
-                cols = slice(piece * (HALF // pieces), (piece + 1) * (HALF // pieces))
-                for c in range(PASSES):
-                    nc.sync.dma_start(out=chunks[c][:, :, cols], in_=chunk_view(half, c, cols))
-            halves.append(chunks)
+        def slice_rows(half, c, i):
+            chunk = halves[half][c]
+            return chunk[:, i] if half == 0 else chunk[:, :, i * SLICE : (i + 1) * SLICE]
 
-        load_half(SLICES)
+        def new_half(shape):
+            halves.append([raw_pool.tile(shape, BF16, tag="raw", name="raw%d" % c) for c in range(PASSES)])
+
+        def load_slice(c, i):
+            cols = slice(i * SLICE, (i + 1) * SLICE)
+            nc.sync.dma_start(out=slice_rows(0, c, i), in_=chunk_view(0, c, cols))
+
+        def load_half():
+            half = len(halves)
+            new_half([P, PACK, HALF])
+            for c in range(PASSES):
+                nc.sync.dma_start(out=halves[half][c][:], in_=chunk_view(half, c, slice(0, HALF)))
+
+        new_half([P, SLICES, PACK, SLICE])
+        for pair in range(PASSES // 2):
+            for c in (2 * pair, 2 * pair + 1):
+                load_slice(c, 0)
+            for bt in (2 * pair, 2 * pair + 1):
+                load_h0(bt)
+        for c in range(PASSES):
+            load_slice(c, 1)
         for i in range(1, HALVES_IN_SBUF):
-            load_half(1)
+            load_half()
 
         ident_f32 = keep.tile([P, P], F32)
         make_identity(nc, ident_f32[:])
@@ -122,7 +137,7 @@ def tile_quantumneuralnetwork_pa_kernel(tc, h0, w1, b1, q1_qw, q1_cw, q1_cb, out
         warm = keep.tile([P, 1], F32)
         nc.scalar.activation(out=warm[:], in_=angle_factor[:, 1, :], func=ACT.Sin)
 
-        nc.vector.memset(small_rows[FILLED_ROWS:P], 0.0)
+        nc.gpsimd.memset(small_rows[FILLED_ROWS:P], 0.0)
         nc.vector.tensor_copy(
             out=small_rows[0:ANGLES], in_=qw_rows[:].rearrange("r q e -> r e q")[:, 0:PACK:3, :]
         )
@@ -152,41 +167,6 @@ def tile_quantumneuralnetwork_pa_kernel(tc, h0, w1, b1, q1_qw, q1_cw, q1_cb, out
             out=args_flat, in0=args_flat, scalar1=-PI_SAFE, scalar2=PI_SAFE,
             op0=ALU.max, op1=ALU.min,
         )
-        sincos = keep.tile([P, 2, 2, DEPTH, H_TILES], F32)
-        nc.scalar.activation(
-            out=sincos[:].rearrange("p f h d m -> p (f h d m)"), in_=args_flat, func=ACT.Sin
-        )
-        nc.scalar.activation(out=warm[:], in_=angle_factor[:, 1, :], func=ACT.Tanh)
-        biases = keep.tile([P, 2, H_TILES], F32)
-        nc.vector.tensor_copy(out=biases[:], in_=small_cols[:, :, ANGLES:FILLED_ROWS])
-
-        def twice(table):
-            return table.unsqueeze(1).to_broadcast([P, 2, H_TILES])
-
-        z0 = sincos[:, COS, THETA, 0, :]
-        yx0 = keep.tile([P, 2, H_TILES], F32)
-        nc.vector.tensor_mul(out=yx0[:], in0=sincos[:, :, PHI, 0, :], in1=twice(sincos[:, SIN, THETA, 0, :]))
-        by_z0 = keep.tile([P, 2, H_TILES], F32)
-        by_x0 = keep.tile([P, 2, H_TILES], F32)
-        nc.vector.tensor_mul(out=by_z0[:], in0=sincos[:, :, THETA, 1, :], in1=twice(z0))
-        nc.vector.tensor_mul(out=by_x0[:], in0=sincos[:, :, THETA, 1, :], in1=twice(yx0[:, 1, :]))
-        y_part = keep.tile([P, H_TILES], F32)
-        nc.vector.tensor_mul(out=y_part[:], in0=yx0[:, 0, :], in1=sincos[:, SIN, PHI, 1, :])
-        xz1 = keep.tile([P, 2, H_TILES], F32)
-        nc.vector.tensor_sub(out=xz1[:, 1, :], in0=by_z0[:, COS, :], in1=by_x0[:, SIN, :])
-        x_part = keep.tile([P, H_TILES], F32)
-        nc.vector.tensor_add(out=x_part[:], in0=by_z0[:, SIN, :], in1=by_x0[:, COS, :])
-        nc.vector.tensor_mul(out=x_part[:], in0=x_part[:], in1=sincos[:, COS, PHI, 1, :])
-        nc.vector.tensor_sub(out=xz1[:, 0, :], in0=x_part[:], in1=y_part[:])
-        by_xz1 = keep.tile([P, 2, H_TILES], F32)
-        nc.vector.tensor_mul(out=by_xz1[:], in0=sincos[:, :, THETA, 2, :], in1=xz1[:])
-        out_bias = keep.tile([P, H_TILES], F32)
-        nc.vector.tensor_sub(out=out_bias[:], in0=by_xz1[:, COS, :], in1=by_xz1[:, SIN, :])
-        nc.vector.tensor_scalar(
-            out=out_bias[:], in0=out_bias[:], scalar1=1.0, scalar2=0.5, op0=ALU.add, op1=ALU.mult
-        )
-        nc.vector.tensor_add(out=out_bias[:], in0=out_bias[:], in1=biases[:, 1, :])
-
         def quantise_pair(grouped, codes, scales, first):
             quantise(
                 nc,
@@ -201,41 +181,33 @@ def tile_quantumneuralnetwork_pa_kernel(tc, h0, w1, b1, q1_qw, q1_cw, q1_cb, out
             bank = psum.tile([P, SLICE], F32, tag="bank", name="bias_bank%d" % n)
             for i in range(SLICE // P):
                 m = n * (SLICE // P) + i
-                nc.tensor.matmul(
-                    out=bank[:, i * P : (i + 1) * P],
-                    lhsT=out_bias[:, m : m + 1].to_broadcast([P, P]),
-                    rhs=ident_f32[:],
-                    start=True,
-                    stop=True,
+                nc.tensor.transpose(
+                    bank[:, i * P : (i + 1) * P], out_bias[:, m : m + 1].to_broadcast([P, P]), ident_f32[:]
                 )
             return bank
 
-        def regroup_pair(step):
+        def regroup_chunk(step, j, grouped, vector_cols):
             group = step // 2
-            first = 2 * (step % 2)
-            chunks = halves[group // SLICES]
-            cols = slice((group % SLICES) * SLICE, (group % SLICES + 1) * SLICE)
-            grouped = grouped_pool.tile([P, 2, SLICE, PACK], BF16, align_bytes=64, tag="grouped")
+            rows = slice_rows(group // SLICES, 2 * (step % 2) + j, group % SLICES)
+            regroup(nc, rows, grouped[:, j], vector_cols)
+
+        def new_grouped():
+            return grouped_pool.tile([P, 2, SLICE, PACK], BF16, align_bytes=64, tag="grouped", name="grouped")
+
+        def regroup_pair(step):
+            grouped = new_grouped()
             for j in range(2):
-                regroup(
-                    nc,
-                    chunks[first + j][:, :, cols],
-                    grouped[:, j],
-                    VECTOR_COLS_1 if group < GROUPS else VECTOR_COLS_2,
-                )
+                regroup_chunk(step, j, grouped, VECTOR_COLS_1 if step < 2 * GROUPS else VECTOR_COLS_2)
             return grouped
 
         h0_words = h0_sb[:].bitcast(F32)
         words_in_pass = K_PASS // 2
         h0_codes = keep.tile([P, PASSES, B], U32, align_bytes=64)
         h0_scales = keep.tile([P, PASSES, B], U8, align_bytes=64)
-        h0_grouped = [
-            grouped_pool.tile([P, 2, B, PACK], BF16, align_bytes=64, tag="grouped", name="h0_grouped%d" % i)
-            for i in range(PASSES // 2)
-        ]
-        for pair in range(B_TILES // 2):
+
+        def transpose_h0(pair):
             for c in range(PASSES):
-                bank = psum.tile([P, 2, 2, P], F32, tag="bank")
+                bank = psum.tile([P, 2, 2, P], F32, tag="bank", name="h0_bank%d" % c)
                 for u in range(2):
                     for i in range(2):
                         nc.tensor.transpose(
@@ -243,14 +215,68 @@ def tile_quantumneuralnetwork_pa_kernel(tc, h0, w1, b1, q1_qw, q1_cw, q1_cb, out
                             h0_words[:, 2 * pair + i, c * words_in_pass + u : (c + 1) * words_in_pass : 2],
                             ident_f32[:],
                         )
-                nc.scalar.copy(
+                copy = nc.scalar.copy if c % 2 == 0 else nc.vector.tensor_copy
+                copy(
                     out=h0_grouped[c // 2][:, c % 2].bitcast(F32)[:, 2 * pair * P : 2 * (pair + 1) * P, :],
                     in_=bank[:].rearrange("p u i b -> p (i b) u"),
                 )
-            if pair == 0:
-                ahead = regroup_pair(0)
+
+        def new_codes():
+            codes = weight_pool.tile([P, PASSES, SLICE], U32, align_bytes=64, tag="codes", name="codes")
+            scales = weight_pool.tile([P, PASSES, SLICE], U8, align_bytes=64, tag="scales", name="scales")
+            return codes, scales
+
+        grouped = new_grouped()
+        h0_grouped = [
+            grouped_pool.tile([P, 2, B, PACK], BF16, align_bytes=64, tag="grouped", name="h0_grouped%d" % i)
+            for i in range(PASSES // 2)
+        ]
+        regroup_chunk(0, 0, grouped, VECTOR_COLS_1)
+        sincos = keep.tile([P, 2, 2, DEPTH, H_TILES], F32)
+        nc.scalar.activation(
+            out=sincos[:].rearrange("p f h d m -> p (f h d m)"), in_=args_flat, func=ACT.Sin
+        )
+        nc.scalar.activation(out=warm[:], in_=angle_factor[:, 1, :], func=ACT.Tanh)
+        regroup_chunk(0, 1, grouped, SLICE)
+        biases = keep.tile([P, 2, H_TILES], F32)
+        nc.vector.tensor_copy(out=biases[:], in_=small_cols[:, :, ANGLES:FILLED_ROWS])
+
+        def twice(table):
+            return table.unsqueeze(1).to_broadcast([P, 2, H_TILES])
+
+        z0 = sincos[:, COS, THETA, 0, :]
+        yx0 = keep.tile([P, 2, H_TILES], F32)
+        nc.gpsimd.tensor_mul(out=yx0[:], in0=sincos[:, :, PHI, 0, :], in1=twice(sincos[:, SIN, THETA, 0, :]))
+        by_z0 = keep.tile([P, 2, H_TILES], F32)
+        by_x0 = keep.tile([P, 2, H_TILES], F32)
+        nc.gpsimd.tensor_mul(out=by_z0[:], in0=sincos[:, :, THETA, 1, :], in1=twice(z0))
+        nc.gpsimd.tensor_mul(out=by_x0[:], in0=sincos[:, :, THETA, 1, :], in1=twice(yx0[:, 1, :]))
+        y_part = keep.tile([P, H_TILES], F32)
+        nc.gpsimd.tensor_mul(out=y_part[:], in0=yx0[:, 0, :], in1=sincos[:, SIN, PHI, 1, :])
+        xz1 = keep.tile([P, 2, H_TILES], F32)
+        nc.gpsimd.tensor_sub(out=xz1[:, 1, :], in0=by_z0[:, COS, :], in1=by_x0[:, SIN, :])
+        x_part = keep.tile([P, H_TILES], F32)
+        nc.gpsimd.tensor_add(out=x_part[:], in0=by_z0[:, SIN, :], in1=by_x0[:, COS, :])
+        nc.gpsimd.tensor_mul(out=x_part[:], in0=x_part[:], in1=sincos[:, COS, PHI, 1, :])
+        nc.gpsimd.tensor_sub(out=xz1[:, 0, :], in0=x_part[:], in1=y_part[:])
+        by_xz1 = keep.tile([P, 2, H_TILES], F32)
+        nc.gpsimd.tensor_mul(out=by_xz1[:], in0=sincos[:, :, THETA, 2, :], in1=xz1[:])
+        out_bias = keep.tile([P, H_TILES], F32)
+        nc.gpsimd.tensor_sub(out=out_bias[:], in0=by_xz1[:, COS, :], in1=by_xz1[:, SIN, :])
+        nc.gpsimd.tensor_scalar(
+            out=out_bias[:], in0=out_bias[:], scalar1=1.0, scalar2=0.5, op0=ALU.add, op1=ALU.mult
+        )
+        nc.gpsimd.tensor_add(out=out_bias[:], in0=out_bias[:], in1=biases[:, 1, :])
+
+        codes, scales = new_codes()
+        quantise_pair(grouped, codes, scales, 0)
+        transpose_h0(0)
+        grouped = regroup_pair(1)
+        quantise_pair(grouped, codes, scales, 2)
+        transpose_h0(1)
         for first in range(0, PASSES, 2):
             quantise_pair(h0_grouped[first // 2], h0_codes, h0_scales, first)
+        ahead = regroup_pair(2)
 
         h1_codes = keep.tile([P, PASSES, B], U32, align_bytes=64)
         h1_scales = keep.tile([P, PASSES, B], U8, align_bytes=64)
@@ -279,45 +305,44 @@ def tile_quantumneuralnetwork_pa_kernel(tc, h0, w1, b1, q1_qw, q1_cw, q1_cb, out
             nc.scalar.activation(out=result[:], in_=result[:], func=ACT.Tanh)
             nc.sync.dma_start(out=out[bt * P : (bt + 1) * P, cols], in_=result[:])
 
-        banks = None
-        h1_rows = None
+        def multiply_first(first, codes, scales, banks):
+            for t in range(PACK):
+                units = slice(t * P, (t + 1) * P)
+                for c in (first, first + 1):
+                    nc.tensor.matmul_mx(
+                        out=banks[t][:],
+                        lhsT=codes[:, c, units].bitcast(FP8X4),
+                        lhsT_scale=scales[:, c, units],
+                        rhs=h0_codes[:, c, :].bitcast(FP8X4),
+                        rhs_scale=h0_scales[:, c, :],
+                        start=(c == 0),
+                        stop=(c == PASSES - 1),
+                    )
+
+        banks = [psum.tile([P, B], F32, tag="bank", name="h1_bank%d" % t) for t in range(PACK)]
+        for first in range(0, PASSES, 2):
+            multiply_first(first, codes, scales, banks)
         bias_bank = None
-        for g in range(GROUPS):
-            codes = weight_pool.tile([P, PASSES, SLICE], U32, align_bytes=64, tag="codes")
-            scales = weight_pool.tile([P, PASSES, SLICE], U8, align_bytes=64, tag="scales")
+        for g in range(1, GROUPS):
+            codes, scales = new_codes()
             last_banks = banks
             banks = [psum.tile([P, B], F32, tag="bank", name="h1_bank%d" % t) for t in range(PACK)]
-            if g > 0:
-                h1_rows = h1_pool.tile([P, PACK, B], BF16, tag="h1_rows")
+            h1_rows = h1_pool.tile([P, PACK, B], BF16, tag="h1_rows")
             for first in range(0, PASSES, 2):
-                pair = (first, first + 1)
                 grouped = ahead
                 ahead = regroup_pair(2 * g + first // 2 + 1)
-                if g > 0:
-                    for i in pair:
-                        relu(h1_rows, g - 1, i, last_banks[i])
-                    bias_bank = bias_rows_step(g - 1, first, bias_bank)
+                for i in (first, first + 1):
+                    relu(h1_rows, g - 1, i, last_banks[i])
+                bias_bank = bias_rows_step(g - 1, first, bias_bank)
                 quantise_pair(grouped, codes, scales, first)
-                if g > 0 and first == PASSES - 2:
+                if first == PASSES - 2:
                     quantise_h1(h1_rows, g - 1)
-                for t in range(PACK):
-                    units = slice(t * P, (t + 1) * P)
-                    for c in pair:
-                        nc.tensor.matmul_mx(
-                            out=banks[t][:],
-                            lhsT=codes[:, c, units].bitcast(FP8X4),
-                            lhsT_scale=scales[:, c, units],
-                            rhs=h0_codes[:, c, :].bitcast(FP8X4),
-                            rhs_scale=h0_scales[:, c, :],
-                            start=(c == 0),
-                            stop=(c == PASSES - 1),
-                        )
+                multiply_first(first, codes, scales, banks)
             if g == SLICES - 1:
-                load_half(1)
+                load_half()
 
         for n in range(GROUPS):
-            codes = weight_pool.tile([P, PASSES, SLICE], U32, align_bytes=64, tag="codes")
-            scales = weight_pool.tile([P, PASSES, SLICE], U8, align_bytes=64, tag="scales")
+            codes, scales = new_codes()
             last_banks = banks
             banks = [psum.tile([P, SLICE], F32, tag="bank", name="out_bank%d" % bt) for bt in range(B_TILES)]
             if n == 0:

@@ -29,14 +29,19 @@ HALF = 1024
 SLICES = HALF // SLICE
 HALVES = H // HALF
 RUN = 4
-VECTOR_COLS_1 = 336
-VECTOR_COLS_2 = 248
+HEAD_VECTOR_COLS = 336
+VECTOR_COLS_1 = 48
+VECTOR_COLS_TURNED = 336
+VECTOR_COLS_ROWS = 0
 HALVES_IN_SBUF = 3
 
 ANGLES = DEPTH * H_TILES
 FILLED_ROWS = ANGLES + H_TILES
 ROUND_MAGIC = 1.5 * 2.0**23
 PI_SAFE = 3.1415925
+
+GROUPS_2 = [(0, 512, False), (512, 1024, True), (1024, 1536, True), (1536, 1792, False), (1792, 2048, False)]
+BIAS_ROWS = [0, 1536]
 
 FLOPS = 2 * (2 * B * H * H)
 
@@ -51,11 +56,12 @@ def by_words(grouped):
 
 def regroup(nc, rows, grouped, vector_cols):
     vector_share = slice(0, vector_cols)
-    scalar_share = slice(vector_cols, SLICE)
-    nc.vector.tensor_copy(
-        out=by_words(grouped[:, vector_share, :]), in_=by_runs(rows[:, :, vector_share])
-    )
-    if vector_cols < SLICE:
+    scalar_share = slice(vector_cols, rows.shape[2])
+    if vector_cols > 0:
+        nc.vector.tensor_copy(
+            out=by_words(grouped[:, vector_share, :]), in_=by_runs(rows[:, :, vector_share])
+        )
+    if vector_cols < rows.shape[2]:
         nc.scalar.copy(out=by_words(grouped[:, scalar_share, :]), in_=by_runs(rows[:, :, scalar_share]))
 
 
@@ -70,10 +76,12 @@ def tile_quantumneuralnetwork_pa_kernel(tc, h0, w1, b1, q1_qw, q1_cw, q1_cb, out
         keep = ctx.enter_context(tc.tile_pool(name="keep", bufs=1))
         raw_pool = ctx.enter_context(tc.tile_pool(name="raw", bufs=HALVES_IN_SBUF * PASSES))
         grouped_pool = ctx.enter_context(tc.tile_pool(name="grouped", bufs=4))
-        weight_pool = ctx.enter_context(tc.tile_pool(name="weight", bufs=3))
+        weight_pool = ctx.enter_context(tc.tile_pool(name="weight", bufs=4))
         h1_pool = ctx.enter_context(tc.tile_pool(name="h1", bufs=2))
-        out_pool = ctx.enter_context(tc.tile_pool(name="out", bufs=4))
-        psum = ctx.enter_context(tc.psum_pool(name="psum", bufs=8))
+        tanh_pool = ctx.enter_context(tc.tile_pool(name="tanh", bufs=5))
+        out_pool = ctx.enter_context(tc.tile_pool(name="out", bufs=3))
+        psum = ctx.enter_context(tc.psum_pool(name="psum", bufs=6))
+        turn_psum = ctx.enter_context(tc.psum_pool(name="turn_psum", bufs=2))
 
         qw_rows = keep.tile([ANGLES, P, PACK], BF16)
         small_rows = keep.tile([P, 2, P], BF16)
@@ -98,16 +106,18 @@ def tile_quantumneuralnetwork_pa_kernel(tc, h0, w1, b1, q1_qw, q1_cw, q1_cb, out
 
         halves = []
 
-        def slice_rows(half, c, i):
+        def weight_rows(half, c, start, width):
             chunk = halves[half][c]
-            return chunk[:, i] if half == 0 else chunk[:, :, i * SLICE : (i + 1) * SLICE]
+            if half == 0:
+                return chunk[:, start // SLICE, :, start % SLICE : start % SLICE + width]
+            return chunk[:, :, start : start + width]
 
         def new_half(shape):
             halves.append([raw_pool.tile(shape, BF16, tag="raw", name="raw%d" % c) for c in range(PASSES)])
 
         def load_slice(c, i):
             cols = slice(i * SLICE, (i + 1) * SLICE)
-            nc.sync.dma_start(out=slice_rows(0, c, i), in_=chunk_view(0, c, cols))
+            nc.sync.dma_start(out=halves[0][c][:, i], in_=chunk_view(0, c, cols))
 
         def load_half():
             half = len(halves)
@@ -175,29 +185,27 @@ def tile_quantumneuralnetwork_pa_kernel(tc, h0, w1, b1, q1_qw, q1_cw, q1_cb, out
                 scales[:, first : first + 2, :].rearrange("p j c -> p (j c)"),
             )
 
-        out_bias_rows = keep.tile([P, H], F32)
+        steps = [
+            (g * SLICE // HALF, g * SLICE % HALF, SLICE, first)
+            for g in range(GROUPS)
+            for first in range(0, PASSES, 2)
+        ]
+        for start, end, is_turned in GROUPS_2:
+            for first in range(0, PASSES, 2):
+                steps.append((HALVES + start // HALF, start % HALF, end - start, first))
 
-        def spread_out_bias(n):
-            bank = psum.tile([P, SLICE], F32, tag="bank", name="bias_bank%d" % n)
-            for i in range(SLICE // P):
-                m = n * (SLICE // P) + i
-                nc.tensor.transpose(
-                    bank[:, i * P : (i + 1) * P], out_bias[:, m : m + 1].to_broadcast([P, P]), ident_f32[:]
-                )
-            return bank
+        def regroup_pass(step, j, grouped, vector_cols):
+            half, start, width, first = steps[step]
+            regroup(nc, weight_rows(half, first + j, start, width), grouped[:, j], vector_cols)
 
-        def regroup_chunk(step, j, grouped, vector_cols):
-            group = step // 2
-            rows = slice_rows(group // SLICES, 2 * (step % 2) + j, group % SLICES)
-            regroup(nc, rows, grouped[:, j], vector_cols)
+        def new_grouped(width):
+            return grouped_pool.tile([P, 2, width, PACK], BF16, align_bytes=64, tag="grouped", name="grouped")
 
-        def new_grouped():
-            return grouped_pool.tile([P, 2, SLICE, PACK], BF16, align_bytes=64, tag="grouped", name="grouped")
-
-        def regroup_pair(step):
-            grouped = new_grouped()
-            for j in range(2):
-                regroup_chunk(step, j, grouped, VECTOR_COLS_1 if step < 2 * GROUPS else VECTOR_COLS_2)
+        def regroup_step(step, vector_cols):
+            width = steps[step][2]
+            grouped = new_grouped(width)
+            regroup_pass(step, 0, grouped, width)
+            regroup_pass(step, 1, grouped, min(vector_cols, width))
             return grouped
 
         h0_words = h0_sb[:].bitcast(F32)
@@ -221,23 +229,24 @@ def tile_quantumneuralnetwork_pa_kernel(tc, h0, w1, b1, q1_qw, q1_cw, q1_cb, out
                     in_=bank[:].rearrange("p u i b -> p (i b) u"),
                 )
 
-        def new_codes():
-            codes = weight_pool.tile([P, PASSES, SLICE], U32, align_bytes=64, tag="codes", name="codes")
-            scales = weight_pool.tile([P, PASSES, SLICE], U8, align_bytes=64, tag="scales", name="scales")
+        def quantise_step(grouped, width):
+            codes = weight_pool.tile([P, 2, width], U32, align_bytes=64, tag="codes", name="codes")
+            scales = weight_pool.tile([P, 2, width], U8, align_bytes=64, tag="scales", name="scales")
+            quantise_pair(grouped, codes, scales, 0)
             return codes, scales
 
-        grouped = new_grouped()
+        grouped = new_grouped(SLICE)
         h0_grouped = [
             grouped_pool.tile([P, 2, B, PACK], BF16, align_bytes=64, tag="grouped", name="h0_grouped%d" % i)
             for i in range(PASSES // 2)
         ]
-        regroup_chunk(0, 0, grouped, VECTOR_COLS_1)
+        regroup_pass(0, 0, grouped, HEAD_VECTOR_COLS)
         sincos = keep.tile([P, 2, 2, DEPTH, H_TILES], F32)
         nc.scalar.activation(
             out=sincos[:].rearrange("p f h d m -> p (f h d m)"), in_=args_flat, func=ACT.Sin
         )
         nc.scalar.activation(out=warm[:], in_=angle_factor[:, 1, :], func=ACT.Tanh)
-        regroup_chunk(0, 1, grouped, SLICE)
+        regroup_pass(0, 1, grouped, SLICE)
         biases = keep.tile([P, 2, H_TILES], F32)
         nc.vector.tensor_copy(out=biases[:], in_=small_cols[:, :, ANGLES:FILLED_ROWS])
 
@@ -268,15 +277,13 @@ def tile_quantumneuralnetwork_pa_kernel(tc, h0, w1, b1, q1_qw, q1_cw, q1_cb, out
         )
         nc.gpsimd.tensor_add(out=out_bias[:], in0=out_bias[:], in1=biases[:, 1, :])
 
-        codes, scales = new_codes()
-        quantise_pair(grouped, codes, scales, 0)
+        quantised = [quantise_step(grouped, SLICE)]
         transpose_h0(0)
-        grouped = regroup_pair(1)
-        quantise_pair(grouped, codes, scales, 2)
+        quantised.append(quantise_step(regroup_step(1, VECTOR_COLS_1), SLICE))
         transpose_h0(1)
         for first in range(0, PASSES, 2):
             quantise_pair(h0_grouped[first // 2], h0_codes, h0_scales, first)
-        ahead = regroup_pair(2)
+        ahead = regroup_step(2, VECTOR_COLS_1)
 
         h1_codes = keep.tile([P, PASSES, B], U32, align_bytes=64)
         h1_scales = keep.tile([P, PASSES, B], U8, align_bytes=64)
@@ -287,32 +294,61 @@ def tile_quantumneuralnetwork_pa_kernel(tc, h0, w1, b1, q1_qw, q1_cw, q1_cb, out
                 out=h1_rows[:, t, :], in_=bank[:], func=ACT.Relu, bias=biases[:, 0, m : m + 1]
             )
 
-        def quantise_h1(h1_rows, g):
-            grouped = h1_pool.tile([P, B, PACK], BF16, align_bytes=64, tag="h1_grouped")
+        def regroup_h1(h1_rows):
+            grouped = h1_pool.tile([P, B, PACK], BF16, align_bytes=64, tag="h1_grouped", name="h1_grouped")
             nc.vector.tensor_copy(out=by_words(grouped[:]), in_=by_runs(h1_rows[:]))
+            return grouped
+
+        def quantise_h1(grouped, g):
             quantise(nc, grouped[:].rearrange("p b t -> p (b t)"), h1_codes[:, g, :], h1_scales[:, g, :])
 
-        def bias_rows_step(n, first, bank):
-            if first == 0:
-                return spread_out_bias(n)
-            nc.scalar.copy(out=out_bias_rows[:, n * SLICE : (n + 1) * SLICE], in_=bank[:])
-            return None
+        out_tiles = out.rearrange("(i b) u -> b i u", b=P)
 
-        def finish_out(n, bt, bank):
-            cols = slice(n * SLICE, (n + 1) * SLICE)
-            result = out_pool.tile([P, SLICE], F32, tag="result")
-            nc.vector.tensor_add(out=result[:], in0=bank[:], in1=out_bias_rows[:, cols])
+        out_bias_rows = keep.tile([P, len(BIAS_ROWS), SLICE], F32)
+
+        def spread_out_bias(n):
+            bank = turn_psum.tile([P, B_TILES, P], F32, tag="turned", name="bias_bank")
+            for i in range(SLICE // P):
+                m = BIAS_ROWS[n] // P + i
+                nc.tensor.transpose(bank[:, i, :], out_bias[:, m : m + 1].to_broadcast([P, P]), ident_f32[:])
+            nc.scalar.copy(
+                out=out_bias_rows[:, n, :], in_=bank[:].rearrange("p i q -> p (i q)")
+            )
+
+        def finish_rows(start, end, bt, bank):
+            result = tanh_pool.tile([P, end - start], F32, tag="result", name="result")
+            n = BIAS_ROWS.index(start // SLICE * SLICE)
+            bias = out_bias_rows[:, n, start % SLICE : start % SLICE + end - start]
+            nc.vector.tensor_add(out=result[:], in0=bank[:], in1=bias)
             nc.scalar.activation(out=result[:], in_=result[:], func=ACT.Tanh)
-            nc.sync.dma_start(out=out[bt * P : (bt + 1) * P, cols], in_=result[:])
+            nc.sync.dma_start(out=out[bt * P : (bt + 1) * P, start:end], in_=result[:])
 
-        def multiply_first(first, codes, scales, banks):
+        def finish(m, bank):
+            result = tanh_pool.tile([P, B], F32, tag="result", name="result")
+            nc.scalar.activation(out=result[:], in_=bank[:], func=ACT.Tanh, bias=out_bias[:, m : m + 1])
+            return result
+
+        def turn(result):
+            turned = turn_psum.tile([P, B_TILES, P], F32, tag="turned", name="turned")
+            for bt in range(B_TILES):
+                nc.tensor.transpose(turned[:, bt, :], result[:, bt * P : (bt + 1) * P], ident_f32[:])
+            return turned
+
+        def store(m, turned, copy):
+            rows = out_pool.tile([P, B_TILES, len(turned) * P], F32, tag="rows", name="rows")
+            for i in range(len(turned)):
+                copy(out=rows[:, :, i * P : (i + 1) * P], in_=turned[i][:])
+            nc.sync.dma_start(out=out_tiles[:, :, m * P : (m + len(turned)) * P], in_=rows[:])
+
+        def multiply_first(first, quantised, banks):
+            codes, scales = quantised
             for t in range(PACK):
                 units = slice(t * P, (t + 1) * P)
                 for c in (first, first + 1):
                     nc.tensor.matmul_mx(
                         out=banks[t][:],
-                        lhsT=codes[:, c, units].bitcast(FP8X4),
-                        lhsT_scale=scales[:, c, units],
+                        lhsT=codes[:, c - first, units].bitcast(FP8X4),
+                        lhsT_scale=scales[:, c - first, units],
                         rhs=h0_codes[:, c, :].bitcast(FP8X4),
                         rhs_scale=h0_scales[:, c, :],
                         start=(c == 0),
@@ -321,58 +357,87 @@ def tile_quantumneuralnetwork_pa_kernel(tc, h0, w1, b1, q1_qw, q1_cw, q1_cb, out
 
         banks = [psum.tile([P, B], F32, tag="bank", name="h1_bank%d" % t) for t in range(PACK)]
         for first in range(0, PASSES, 2):
-            multiply_first(first, codes, scales, banks)
-        bias_bank = None
+            multiply_first(first, quantised[first // 2], banks)
         for g in range(1, GROUPS):
-            codes, scales = new_codes()
             last_banks = banks
             banks = [psum.tile([P, B], F32, tag="bank", name="h1_bank%d" % t) for t in range(PACK)]
             h1_rows = h1_pool.tile([P, PACK, B], BF16, tag="h1_rows")
             for first in range(0, PASSES, 2):
                 grouped = ahead
-                ahead = regroup_pair(2 * g + first // 2 + 1)
-                for i in (first, first + 1):
-                    relu(h1_rows, g - 1, i, last_banks[i])
-                bias_bank = bias_rows_step(g - 1, first, bias_bank)
-                quantise_pair(grouped, codes, scales, first)
-                if first == PASSES - 2:
-                    quantise_h1(h1_rows, g - 1)
-                multiply_first(first, codes, scales, banks)
+                ahead = regroup_step(2 * g + first // 2 + 1, VECTOR_COLS_1)
+                if first == 0:
+                    for t in range(PACK):
+                        relu(h1_rows, g - 1, t, last_banks[t])
+                else:
+                    h1_grouped = regroup_h1(h1_rows)
+                    if g > 1:
+                        spread_out_bias(g - 2)
+                quantised = quantise_step(grouped, SLICE)
+                if first > 0:
+                    quantise_h1(h1_grouped, g - 1)
+                multiply_first(first, quantised, banks)
             if g == SLICES - 1:
                 load_half()
 
-        for n in range(GROUPS):
-            codes, scales = new_codes()
+        step = 2 * GROUPS
+        done = []
+        turned = []
+        turned_m = 0
+        h1_rows = h1_pool.tile([P, PACK, B], BF16, tag="h1_rows")
+        for start, end, is_turned in GROUPS_2:
+            width = end - start
+            tiles = width // P if is_turned else B_TILES
+            tile_cols = B if is_turned else width
             last_banks = banks
-            banks = [psum.tile([P, SLICE], F32, tag="bank", name="out_bank%d" % bt) for bt in range(B_TILES)]
-            if n == 0:
-                h1_rows = h1_pool.tile([P, PACK, B], BF16, tag="h1_rows")
+            banks = [psum.tile([P, tile_cols], F32, tag="bank", name="out_bank%d" % t) for t in range(tiles)]
             for first in range(0, PASSES, 2):
-                pair = (first, first + 1)
                 grouped = ahead
-                if n < GROUPS - 1 or first < PASSES - 2:
-                    ahead = regroup_pair(2 * (GROUPS + n) + first // 2 + 1)
-                for i in pair:
-                    if n == 0:
-                        relu(h1_rows, GROUPS - 1, i, last_banks[i])
+                if start == 0 and first == 0:
+                    for t in range(PACK):
+                        relu(h1_rows, GROUPS - 1, t, last_banks[t])
+                if start == 0 and first > 0:
+                    h1_grouped = regroup_h1(h1_rows)
+                    codes, scales = quantise_step(grouped, width)
+                    quantise_h1(h1_grouped, GROUPS - 1)
+                vector_cols = VECTOR_COLS_1 if start == 0 else VECTOR_COLS_TURNED if done[0][0] else VECTOR_COLS_ROWS
+                if step + 1 < len(steps):
+                    ahead = regroup_step(step + 1, vector_cols)
+                part = done[0 : len(done) // 2] if first == 0 else done[len(done) // 2 :]
+                results = []
+                for kind, where, bank in part:
+                    if kind:
+                        results.append(finish(where, bank))
                     else:
-                        finish_out(n - 1, i, last_banks[i])
-                if n == 0:
-                    bias_bank = bias_rows_step(GROUPS - 1, first, bias_bank)
-                quantise_pair(grouped, codes, scales, first)
-                if n == 0 and first == PASSES - 2:
-                    quantise_h1(h1_rows, GROUPS - 1)
-                for bt in range(B_TILES):
-                    rows = slice(bt * P, (bt + 1) * P)
-                    for g in pair:
+                        finish_rows(where[0], where[1], where[2], bank)
+                if turned:
+                    store(turned_m, turned, nc.scalar.copy)
+                    turned = []
+                if start > 0 or first == 0:
+                    codes, scales = quantise_step(grouped, width)
+                for t in range(tiles):
+                    if t == tiles // 2 and results:
+                        turned = [turn(result) for result in results]
+                        turned_m = part[0][1]
+                    part_of_tile = slice(t * P, (t + 1) * P)
+                    for g in (first, first + 1):
+                        if is_turned:
+                            lhs, lhs_scales = codes[:, g - first, part_of_tile], scales[:, g - first, part_of_tile]
+                            rhs, rhs_scales = h1_codes[:, g, :], h1_scales[:, g, :]
+                        else:
+                            lhs, lhs_scales = h1_codes[:, g, part_of_tile], h1_scales[:, g, part_of_tile]
+                            rhs, rhs_scales = codes[:, g - first, :], scales[:, g - first, :]
                         nc.tensor.matmul_mx(
-                            out=banks[bt][:],
-                            lhsT=h1_codes[:, g, rows].bitcast(FP8X4),
-                            lhsT_scale=h1_scales[:, g, rows],
-                            rhs=codes[:, g, :].bitcast(FP8X4),
-                            rhs_scale=scales[:, g, :],
+                            out=banks[t][:],
+                            lhsT=lhs.bitcast(FP8X4),
+                            lhsT_scale=lhs_scales,
+                            rhs=rhs.bitcast(FP8X4),
+                            rhs_scale=rhs_scales,
                             start=(g == 0),
                             stop=(g == PASSES - 1),
                         )
-        for bt in range(B_TILES):
-            finish_out(GROUPS - 1, bt, banks[bt])
+                step += 1
+            done = [
+                (is_turned, start // P + t if is_turned else (start, end, t), banks[t]) for t in range(tiles)
+            ]
+        for kind, where, bank in done:
+            finish_rows(where[0], where[1], where[2], bank)

@@ -28,11 +28,10 @@ GROUPS = H // SLICE
 HALF = 1024
 SLICES = HALF // SLICE
 HALVES = H // HALF
-RUN = 4
+RUN = 8
 HEAD_VECTOR_COLS = 336
 VECTOR_COLS_1 = 48
-VECTOR_COLS_TURNED = 336
-VECTOR_COLS_ROWS = 0
+VECTOR_COLS_2 = 0
 HALVES_IN_SBUF = 3
 
 ANGLES = DEPTH * H_TILES
@@ -40,8 +39,7 @@ FILLED_ROWS = ANGLES + H_TILES
 ROUND_MAGIC = 1.5 * 2.0**23
 PI_SAFE = 3.1415925
 
-GROUPS_2 = [(0, 512, False), (512, 1024, True), (1024, 1536, True), (1536, 1792, False), (1792, 2048, False)]
-BIAS_ROWS = [0, 1536]
+GROUPS_2 = [(0, 512), (512, 1024), (1024, 1536), (1536, 1792), (1792, 2048)]
 
 FLOPS = 2 * (2 * B * H * H)
 
@@ -78,10 +76,9 @@ def tile_quantumneuralnetwork_pa_kernel(tc, h0, w1, b1, q1_qw, q1_cw, q1_cb, out
         grouped_pool = ctx.enter_context(tc.tile_pool(name="grouped", bufs=4))
         weight_pool = ctx.enter_context(tc.tile_pool(name="weight", bufs=4))
         h1_pool = ctx.enter_context(tc.tile_pool(name="h1", bufs=2))
-        tanh_pool = ctx.enter_context(tc.tile_pool(name="tanh", bufs=5))
-        out_pool = ctx.enter_context(tc.tile_pool(name="out", bufs=3))
+        out_pool = ctx.enter_context(tc.tile_pool(name="out", bufs=8))
         psum = ctx.enter_context(tc.psum_pool(name="psum", bufs=6))
-        turn_psum = ctx.enter_context(tc.psum_pool(name="turn_psum", bufs=2))
+        spread_psum = ctx.enter_context(tc.psum_pool(name="spread_psum", bufs=2))
 
         qw_rows = keep.tile([ANGLES, P, PACK], BF16)
         small_rows = keep.tile([P, 2, P], BF16)
@@ -107,25 +104,24 @@ def tile_quantumneuralnetwork_pa_kernel(tc, h0, w1, b1, q1_qw, q1_cw, q1_cb, out
         halves = []
 
         def weight_rows(half, c, start, width):
-            chunk = halves[half][c]
-            if half == 0:
-                return chunk[:, start // SLICE, :, start % SLICE : start % SLICE + width]
-            return chunk[:, :, start : start + width]
+            return halves[half][c][:, start // SLICE, :, start % SLICE : start % SLICE + width]
 
-        def new_half(shape):
-            halves.append([raw_pool.tile(shape, BF16, tag="raw", name="raw%d" % c) for c in range(PASSES)])
+        def new_half():
+            halves.append(
+                [raw_pool.tile([P, SLICES, PACK, SLICE], BF16, tag="raw", name="raw%d" % c) for c in range(PASSES)]
+            )
 
         def load_slice(c, i):
             cols = slice(i * SLICE, (i + 1) * SLICE)
-            nc.sync.dma_start(out=halves[0][c][:, i], in_=chunk_view(0, c, cols))
+            nc.sync.dma_start(out=halves[-1][c][:, i], in_=chunk_view(len(halves) - 1, c, cols))
 
         def load_half():
-            half = len(halves)
-            new_half([P, PACK, HALF])
-            for c in range(PASSES):
-                nc.sync.dma_start(out=halves[half][c][:], in_=chunk_view(half, c, slice(0, HALF)))
+            new_half()
+            for i in range(SLICES):
+                for c in range(PASSES):
+                    load_slice(c, i)
 
-        new_half([P, SLICES, PACK, SLICE])
+        new_half()
         for pair in range(PASSES // 2):
             for c in (2 * pair, 2 * pair + 1):
                 load_slice(c, 0)
@@ -190,7 +186,7 @@ def tile_quantumneuralnetwork_pa_kernel(tc, h0, w1, b1, q1_qw, q1_cw, q1_cb, out
             for g in range(GROUPS)
             for first in range(0, PASSES, 2)
         ]
-        for start, end, is_turned in GROUPS_2:
+        for start, end in GROUPS_2:
             for first in range(0, PASSES, 2):
                 steps.append((HALVES + start // HALF, start % HALF, end - start, first))
 
@@ -302,43 +298,22 @@ def tile_quantumneuralnetwork_pa_kernel(tc, h0, w1, b1, q1_qw, q1_cw, q1_cb, out
         def quantise_h1(grouped, g):
             quantise(nc, grouped[:].rearrange("p b t -> p (b t)"), h1_codes[:, g, :], h1_scales[:, g, :])
 
-        out_tiles = out.rearrange("(i b) u -> b i u", b=P)
-
-        out_bias_rows = keep.tile([P, len(BIAS_ROWS), SLICE], F32)
+        out_bias_rows = keep.tile([P, H], F32)
 
         def spread_out_bias(n):
-            bank = turn_psum.tile([P, B_TILES, P], F32, tag="turned", name="bias_bank")
+            bank = spread_psum.tile([P, SLICE], F32, tag="spread", name="bias_bank")
             for i in range(SLICE // P):
-                m = BIAS_ROWS[n] // P + i
-                nc.tensor.transpose(bank[:, i, :], out_bias[:, m : m + 1].to_broadcast([P, P]), ident_f32[:])
-            nc.scalar.copy(
-                out=out_bias_rows[:, n, :], in_=bank[:].rearrange("p i q -> p (i q)")
-            )
+                m = n * (SLICE // P) + i
+                nc.tensor.transpose(
+                    bank[:, i * P : (i + 1) * P], out_bias[:, m : m + 1].to_broadcast([P, P]), ident_f32[:]
+                )
+            nc.scalar.copy(out=out_bias_rows[:, n * SLICE : (n + 1) * SLICE], in_=bank[:])
 
-        def finish_rows(start, end, bt, bank):
-            result = tanh_pool.tile([P, end - start], F32, tag="result", name="result")
-            n = BIAS_ROWS.index(start // SLICE * SLICE)
-            bias = out_bias_rows[:, n, start % SLICE : start % SLICE + end - start]
-            nc.vector.tensor_add(out=result[:], in0=bank[:], in1=bias)
+        def finish_out(start, end, bt, bank):
+            result = out_pool.tile([P, end - start], F32, tag="result", name="result")
+            nc.vector.tensor_add(out=result[:], in0=bank[:], in1=out_bias_rows[:, start:end])
             nc.scalar.activation(out=result[:], in_=result[:], func=ACT.Tanh)
             nc.sync.dma_start(out=out[bt * P : (bt + 1) * P, start:end], in_=result[:])
-
-        def finish(m, bank):
-            result = tanh_pool.tile([P, B], F32, tag="result", name="result")
-            nc.scalar.activation(out=result[:], in_=bank[:], func=ACT.Tanh, bias=out_bias[:, m : m + 1])
-            return result
-
-        def turn(result):
-            turned = turn_psum.tile([P, B_TILES, P], F32, tag="turned", name="turned")
-            for bt in range(B_TILES):
-                nc.tensor.transpose(turned[:, bt, :], result[:, bt * P : (bt + 1) * P], ident_f32[:])
-            return turned
-
-        def store(m, turned, copy):
-            rows = out_pool.tile([P, B_TILES, len(turned) * P], F32, tag="rows", name="rows")
-            for i in range(len(turned)):
-                copy(out=rows[:, :, i * P : (i + 1) * P], in_=turned[i][:])
-            nc.sync.dma_start(out=out_tiles[:, :, m * P : (m + len(turned)) * P], in_=rows[:])
 
         def multiply_first(first, quantised, banks):
             codes, scales = quantised
@@ -370,8 +345,7 @@ def tile_quantumneuralnetwork_pa_kernel(tc, h0, w1, b1, q1_qw, q1_cw, q1_cb, out
                         relu(h1_rows, g - 1, t, last_banks[t])
                 else:
                     h1_grouped = regroup_h1(h1_rows)
-                    if g > 1:
-                        spread_out_bias(g - 2)
+                    spread_out_bias(g - 1)
                 quantised = quantise_step(grouped, SLICE)
                 if first > 0:
                     quantise_h1(h1_grouped, g - 1)
@@ -381,15 +355,11 @@ def tile_quantumneuralnetwork_pa_kernel(tc, h0, w1, b1, q1_qw, q1_cw, q1_cb, out
 
         step = 2 * GROUPS
         done = []
-        turned = []
-        turned_m = 0
         h1_rows = h1_pool.tile([P, PACK, B], BF16, tag="h1_rows")
-        for start, end, is_turned in GROUPS_2:
+        for start, end in GROUPS_2:
             width = end - start
-            tiles = width // P if is_turned else B_TILES
-            tile_cols = B if is_turned else width
             last_banks = banks
-            banks = [psum.tile([P, tile_cols], F32, tag="bank", name="out_bank%d" % t) for t in range(tiles)]
+            banks = [psum.tile([P, width], F32, tag="bank", name="out_bank%d" % bt) for bt in range(B_TILES)]
             for first in range(0, PASSES, 2):
                 grouped = ahead
                 if start == 0 and first == 0:
@@ -399,45 +369,27 @@ def tile_quantumneuralnetwork_pa_kernel(tc, h0, w1, b1, q1_qw, q1_cw, q1_cb, out
                     h1_grouped = regroup_h1(h1_rows)
                     codes, scales = quantise_step(grouped, width)
                     quantise_h1(h1_grouped, GROUPS - 1)
-                vector_cols = VECTOR_COLS_1 if start == 0 else VECTOR_COLS_TURNED if done[0][0] else VECTOR_COLS_ROWS
                 if step + 1 < len(steps):
-                    ahead = regroup_step(step + 1, vector_cols)
-                part = done[0 : len(done) // 2] if first == 0 else done[len(done) // 2 :]
-                results = []
-                for kind, where, bank in part:
-                    if kind:
-                        results.append(finish(where, bank))
-                    else:
-                        finish_rows(where[0], where[1], where[2], bank)
-                if turned:
-                    store(turned_m, turned, nc.scalar.copy)
-                    turned = []
+                    ahead = regroup_step(step + 1, VECTOR_COLS_1 if start == 0 else VECTOR_COLS_2)
+                if start == 0 and first > 0:
+                    spread_out_bias(GROUPS - 1)
+                for tile in done[first : first + 2]:
+                    finish_out(*tile)
                 if start > 0 or first == 0:
                     codes, scales = quantise_step(grouped, width)
-                for t in range(tiles):
-                    if t == tiles // 2 and results:
-                        turned = [turn(result) for result in results]
-                        turned_m = part[0][1]
-                    part_of_tile = slice(t * P, (t + 1) * P)
+                for bt in range(B_TILES):
+                    rows = slice(bt * P, (bt + 1) * P)
                     for g in (first, first + 1):
-                        if is_turned:
-                            lhs, lhs_scales = codes[:, g - first, part_of_tile], scales[:, g - first, part_of_tile]
-                            rhs, rhs_scales = h1_codes[:, g, :], h1_scales[:, g, :]
-                        else:
-                            lhs, lhs_scales = h1_codes[:, g, part_of_tile], h1_scales[:, g, part_of_tile]
-                            rhs, rhs_scales = codes[:, g - first, :], scales[:, g - first, :]
                         nc.tensor.matmul_mx(
-                            out=banks[t][:],
-                            lhsT=lhs.bitcast(FP8X4),
-                            lhsT_scale=lhs_scales,
-                            rhs=rhs.bitcast(FP8X4),
-                            rhs_scale=rhs_scales,
+                            out=banks[bt][:],
+                            lhsT=h1_codes[:, g, rows].bitcast(FP8X4),
+                            lhsT_scale=h1_scales[:, g, rows],
+                            rhs=codes[:, g - first, :].bitcast(FP8X4),
+                            rhs_scale=scales[:, g - first, :],
                             start=(g == 0),
                             stop=(g == PASSES - 1),
                         )
                 step += 1
-            done = [
-                (is_turned, start // P + t if is_turned else (start, end, t), banks[t]) for t in range(tiles)
-            ]
-        for kind, where, bank in done:
-            finish_rows(where[0], where[1], where[2], bank)
+            done = [(start, end, bt, banks[bt]) for bt in range(B_TILES)]
+        for tile in done:
+            finish_out(*tile)

@@ -28,10 +28,11 @@ GROUPS = H // SLICE
 HALF = 1024
 SLICES = HALF // SLICE
 HALVES = H // HALF
-RUN = 8
+RUN = 4
 HEAD_VECTOR_COLS = 336
 VECTOR_COLS_1 = 48
-VECTOR_COLS_2 = 0
+VECTOR_COLS_TURNED = 256
+VECTOR_COLS_ROWS = 0
 HALVES_IN_SBUF = 3
 
 ANGLES = DEPTH * H_TILES
@@ -39,7 +40,8 @@ FILLED_ROWS = ANGLES + H_TILES
 ROUND_MAGIC = 1.5 * 2.0**23
 PI_SAFE = 3.1415925
 
-GROUPS_2 = [(0, 512), (512, 1024), (1024, 1536), (1536, 1792), (1792, 2048)]
+GROUPS_2 = [(0, 512, True), (512, 1024, False), (1024, 1536, True), (1536, 1792, False), (1792, 2048, False)]
+BIAS_ROWS = [512, 1536]
 
 FLOPS = 2 * (2 * B * H * H)
 
@@ -76,9 +78,10 @@ def tile_quantumneuralnetwork_pa_kernel(tc, h0, w1, b1, q1_qw, q1_cw, q1_cb, out
         grouped_pool = ctx.enter_context(tc.tile_pool(name="grouped", bufs=4))
         weight_pool = ctx.enter_context(tc.tile_pool(name="weight", bufs=4))
         h1_pool = ctx.enter_context(tc.tile_pool(name="h1", bufs=2))
-        out_pool = ctx.enter_context(tc.tile_pool(name="out", bufs=8))
+        tanh_pool = ctx.enter_context(tc.tile_pool(name="tanh", bufs=7))
+        out_pool = ctx.enter_context(tc.tile_pool(name="out", bufs=3))
         psum = ctx.enter_context(tc.psum_pool(name="psum", bufs=6))
-        spread_psum = ctx.enter_context(tc.psum_pool(name="spread_psum", bufs=2))
+        turn_psum = ctx.enter_context(tc.psum_pool(name="turn_psum", bufs=2))
 
         qw_rows = keep.tile([ANGLES, P, PACK], BF16)
         small_rows = keep.tile([P, 2, P], BF16)
@@ -97,7 +100,7 @@ def tile_quantumneuralnetwork_pa_kernel(tc, h0, w1, b1, q1_qw, q1_cw, q1_cb, out
         def chunk_view(half, c, cols):
             if half < HALVES:
                 rows = w1[c * K_PASS : (c + 1) * K_PASS, half * HALF : (half + 1) * HALF]
-                return rows.rearrange("(p t) n -> p t n", t=PACK)[:, :, cols]
+                return rows.rearrange("(u p e) n -> u p e n", u=2, e=2)[:, :, :, cols]
             rows = q1_cw[c * K_PASS : (c + 1) * K_PASS, (half - HALVES) * HALF : (half - HALVES + 1) * HALF]
             return rows.rearrange("(t p) n -> p t n", p=P)[:, :, cols]
 
@@ -113,7 +116,13 @@ def tile_quantumneuralnetwork_pa_kernel(tc, h0, w1, b1, q1_qw, q1_cw, q1_cb, out
 
         def load_slice(c, i):
             cols = slice(i * SLICE, (i + 1) * SLICE)
-            nc.sync.dma_start(out=halves[-1][c][:, i], in_=chunk_view(len(halves) - 1, c, cols))
+            view = chunk_view(len(halves) - 1, c, cols)
+            tile = halves[-1][c][:, i]
+            if len(halves) <= HALVES:
+                for u in range(2):
+                    nc.sync.dma_start(out=tile[:, 2 * u : 2 * u + 2, :], in_=view[u])
+            else:
+                nc.sync.dma_start(out=tile, in_=view)
 
         def load_half():
             new_half()
@@ -186,7 +195,7 @@ def tile_quantumneuralnetwork_pa_kernel(tc, h0, w1, b1, q1_qw, q1_cw, q1_cb, out
             for g in range(GROUPS)
             for first in range(0, PASSES, 2)
         ]
-        for start, end in GROUPS_2:
+        for start, end, is_turned in GROUPS_2:
             for first in range(0, PASSES, 2):
                 steps.append((HALVES + start // HALF, start % HALF, end - start, first))
 
@@ -216,7 +225,7 @@ def tile_quantumneuralnetwork_pa_kernel(tc, h0, w1, b1, q1_qw, q1_cw, q1_cb, out
                     for i in range(2):
                         nc.tensor.transpose(
                             bank[:, u, i, :],
-                            h0_words[:, 2 * pair + i, c * words_in_pass + u : (c + 1) * words_in_pass : 2],
+                            h0_words[:, 2 * pair + i, c * words_in_pass + u * P : c * words_in_pass + (u + 1) * P],
                             ident_f32[:],
                         )
                 copy = nc.scalar.copy if c % 2 == 0 else nc.vector.tensor_copy
@@ -298,22 +307,43 @@ def tile_quantumneuralnetwork_pa_kernel(tc, h0, w1, b1, q1_qw, q1_cw, q1_cb, out
         def quantise_h1(grouped, g):
             quantise(nc, grouped[:].rearrange("p b t -> p (b t)"), h1_codes[:, g, :], h1_scales[:, g, :])
 
-        out_bias_rows = keep.tile([P, H], F32)
+        out_tiles = out.rearrange("(i b) u -> b i u", b=P)
+
+        out_bias_rows = keep.tile([P, len(BIAS_ROWS), SLICE], F32)
 
         def spread_out_bias(n):
-            bank = spread_psum.tile([P, SLICE], F32, tag="spread", name="bias_bank")
+            bank = turn_psum.tile([P, B_TILES, P], F32, tag="turned", name="bias_bank")
             for i in range(SLICE // P):
-                m = n * (SLICE // P) + i
-                nc.tensor.transpose(
-                    bank[:, i * P : (i + 1) * P], out_bias[:, m : m + 1].to_broadcast([P, P]), ident_f32[:]
-                )
-            nc.scalar.copy(out=out_bias_rows[:, n * SLICE : (n + 1) * SLICE], in_=bank[:])
+                m = BIAS_ROWS[n] // P + i
+                nc.tensor.transpose(bank[:, i, :], out_bias[:, m : m + 1].to_broadcast([P, P]), ident_f32[:])
+            nc.scalar.copy(
+                out=out_bias_rows[:, n, :], in_=bank[:].rearrange("p i q -> p (i q)")
+            )
 
-        def finish_out(start, end, bt, bank):
-            result = out_pool.tile([P, end - start], F32, tag="result", name="result")
-            nc.vector.tensor_add(out=result[:], in0=bank[:], in1=out_bias_rows[:, start:end])
+        def finish_rows(start, end, bt, bank):
+            result = tanh_pool.tile([P, end - start], F32, tag="result", name="result")
+            n = BIAS_ROWS.index(start // SLICE * SLICE)
+            bias = out_bias_rows[:, n, start % SLICE : start % SLICE + end - start]
+            nc.vector.tensor_add(out=result[:], in0=bank[:], in1=bias)
             nc.scalar.activation(out=result[:], in_=result[:], func=ACT.Tanh)
             nc.sync.dma_start(out=out[bt * P : (bt + 1) * P, start:end], in_=result[:])
+
+        def finish(m, bank):
+            result = tanh_pool.tile([P, B], F32, tag="result", name="result")
+            nc.scalar.activation(out=result[:], in_=bank[:], func=ACT.Tanh, bias=out_bias[:, m : m + 1])
+            return result
+
+        def turn(result):
+            turned = turn_psum.tile([P, B_TILES, P], F32, tag="turned", name="turned")
+            for bt in range(B_TILES):
+                nc.tensor.transpose(turned[:, bt, :], result[:, bt * P : (bt + 1) * P], ident_f32[:])
+            return turned
+
+        def store(m, turned, copy):
+            rows = out_pool.tile([P, B_TILES, len(turned) * P], F32, tag="rows", name="rows")
+            for i in range(len(turned)):
+                copy(out=rows[:, :, i * P : (i + 1) * P], in_=turned[i][:])
+            nc.sync.dma_start(out=out_tiles[:, :, m * P : (m + len(turned)) * P], in_=rows[:])
 
         def multiply_first(first, quantised, banks):
             codes, scales = quantised
@@ -345,7 +375,9 @@ def tile_quantumneuralnetwork_pa_kernel(tc, h0, w1, b1, q1_qw, q1_cw, q1_cb, out
                         relu(h1_rows, g - 1, t, last_banks[t])
                 else:
                     h1_grouped = regroup_h1(h1_rows)
-                    spread_out_bias(g - 1)
+                    if g > 1:
+                        for n in range(g - 2, len(BIAS_ROWS), 2):
+                            spread_out_bias(n)
                 quantised = quantise_step(grouped, SLICE)
                 if first > 0:
                     quantise_h1(h1_grouped, g - 1)
@@ -355,11 +387,15 @@ def tile_quantumneuralnetwork_pa_kernel(tc, h0, w1, b1, q1_qw, q1_cw, q1_cb, out
 
         step = 2 * GROUPS
         done = []
+        turned = []
+        turned_m = 0
         h1_rows = h1_pool.tile([P, PACK, B], BF16, tag="h1_rows")
-        for start, end in GROUPS_2:
+        for start, end, is_turned in GROUPS_2:
             width = end - start
+            tiles = width // P if is_turned else B_TILES
+            tile_cols = B if is_turned else width
             last_banks = banks
-            banks = [psum.tile([P, width], F32, tag="bank", name="out_bank%d" % bt) for bt in range(B_TILES)]
+            banks = [psum.tile([P, tile_cols], F32, tag="bank", name="out_bank%d" % t) for t in range(tiles)]
             for first in range(0, PASSES, 2):
                 grouped = ahead
                 if start == 0 and first == 0:
@@ -369,27 +405,47 @@ def tile_quantumneuralnetwork_pa_kernel(tc, h0, w1, b1, q1_qw, q1_cw, q1_cb, out
                     h1_grouped = regroup_h1(h1_rows)
                     codes, scales = quantise_step(grouped, width)
                     quantise_h1(h1_grouped, GROUPS - 1)
+                vector_cols = VECTOR_COLS_1 if start == 0 else VECTOR_COLS_TURNED if done[0][0] else VECTOR_COLS_ROWS
                 if step + 1 < len(steps):
-                    ahead = regroup_step(step + 1, VECTOR_COLS_1 if start == 0 else VECTOR_COLS_2)
-                if start == 0 and first > 0:
-                    spread_out_bias(GROUPS - 1)
-                for tile in done[first : first + 2]:
-                    finish_out(*tile)
+                    ahead = regroup_step(step + 1, vector_cols)
+                part = done[0 : len(done) // 2] if first == 0 else done[len(done) // 2 :]
+                results = []
+                for kind, where, bank in part:
+                    if kind:
+                        results.append(finish(where, bank))
+                    else:
+                        finish_rows(where[0], where[1], where[2], bank)
+                if turned:
+                    store(turned_m, turned, nc.scalar.copy)
+                    turned = []
                 if start > 0 or first == 0:
                     codes, scales = quantise_step(grouped, width)
-                for bt in range(B_TILES):
-                    rows = slice(bt * P, (bt + 1) * P)
+                for t in range(tiles):
+                    if t == tiles // 2 and results:
+                        turned = [turn(result) for result in results]
+                        turned_m = part[0][1]
+                    part_of_tile = slice(t * P, (t + 1) * P)
                     for g in (first, first + 1):
+                        if is_turned:
+                            lhs, lhs_scales = codes[:, g - first, part_of_tile], scales[:, g - first, part_of_tile]
+                            rhs, rhs_scales = h1_codes[:, g, :], h1_scales[:, g, :]
+                        else:
+                            lhs, lhs_scales = h1_codes[:, g, part_of_tile], h1_scales[:, g, part_of_tile]
+                            rhs, rhs_scales = codes[:, g - first, :], scales[:, g - first, :]
                         nc.tensor.matmul_mx(
-                            out=banks[bt][:],
-                            lhsT=h1_codes[:, g, rows].bitcast(FP8X4),
-                            lhsT_scale=h1_scales[:, g, rows],
-                            rhs=codes[:, g - first, :].bitcast(FP8X4),
-                            rhs_scale=scales[:, g - first, :],
+                            out=banks[t][:],
+                            lhsT=lhs.bitcast(FP8X4),
+                            lhsT_scale=lhs_scales,
+                            rhs=rhs.bitcast(FP8X4),
+                            rhs_scale=rhs_scales,
                             start=(g == 0),
                             stop=(g == PASSES - 1),
                         )
                 step += 1
-            done = [(start, end, bt, banks[bt]) for bt in range(B_TILES)]
-        for tile in done:
-            finish_out(*tile)
+            done = [
+                (is_turned, start // P + t if is_turned else (start, end, t), banks[t]) for t in range(tiles)
+            ]
+        if turned:
+            store(turned_m, turned, nc.vector.tensor_copy)
+        for kind, where, bank in done:
+            finish_rows(where[0], where[1], where[2], bank)

@@ -160,6 +160,15 @@ def tile_quantumneuralnetwork_pa_kernel(tc, h0, w1, b1, q1_qw, q1_cw, q1_cb, out
         for h in range(2):
             nc.tensor.transpose(small_cols[:, h, :], small_rows[:, h, :], ident_bf16[:])
 
+        zeros = keep.tile([P, SLICE], BF16)
+        nc.gpsimd.memset(zeros[:], 0.0)
+
+        def warm_up(products):
+            bank = turn_psum.tile([P, SLICE], F32, tag="turned", name="warm_bank")
+            for i in range(products):
+                nc.tensor.matmul(out=bank[:], lhsT=ident_bf16[:], rhs=zeros[:], start=True, stop=True)
+
+        warm_up(8)
         args = keep.tile([P, 2, 2, ANGLES], F32)
         nc.vector.tensor_mul(
             out=args[:, 0],
@@ -284,8 +293,10 @@ def tile_quantumneuralnetwork_pa_kernel(tc, h0, w1, b1, q1_qw, q1_cw, q1_cb, out
 
         quantised = [quantise_step(grouped, SLICE)]
         transpose_h0(0)
+        warm_up(6)
         quantised.append(quantise_step(regroup_step(1, VECTOR_COLS_1), SLICE))
         transpose_h0(1)
+        warm_up(2)
         for first in range(0, PASSES, 2):
             quantise_pair(h0_grouped[first // 2], h0_codes, h0_scales, first)
         ahead = regroup_step(2, VECTOR_COLS_1)

@@ -43,6 +43,8 @@ PI_SAFE = 3.1415925
 GROUPS_2 = [(0, 512, True), (512, 1024, False), (1024, 1536, True), (1536, 1792, False), (1792, 2048, False)]
 BIAS_ROWS = [512, 1536]
 
+FILL = {1: 2, 2: 2, 3: 2, 4: 2, 5: 2, 6: 2, 7: 2, 9: 6}
+
 FLOPS = 2 * (2 * B * H * H)
 
 
@@ -164,6 +166,8 @@ def tile_quantumneuralnetwork_pa_kernel(tc, h0, w1, b1, q1_qw, q1_cw, q1_cb, out
         nc.gpsimd.memset(zeros[:], 0.0)
 
         def warm_up(products):
+            if products == 0:
+                return
             bank = turn_psum.tile([P, SLICE], F32, tag="turned", name="warm_bank")
             for i in range(products):
                 nc.tensor.matmul(out=bank[:], lhsT=ident_bf16[:], rhs=zeros[:], start=True, stop=True)
@@ -374,6 +378,7 @@ def tile_quantumneuralnetwork_pa_kernel(tc, h0, w1, b1, q1_qw, q1_cw, q1_cb, out
         banks = [psum.tile([P, B], F32, tag="bank", name="h1_bank%d" % t) for t in range(PACK)]
         for first in range(0, PASSES, 2):
             multiply_first(first, quantised[first // 2], banks)
+            warm_up(FILL.get(first // 2, 0))
         for g in range(1, GROUPS):
             last_banks = banks
             banks = [psum.tile([P, B], F32, tag="bank", name="h1_bank%d" % t) for t in range(PACK)]
@@ -393,6 +398,7 @@ def tile_quantumneuralnetwork_pa_kernel(tc, h0, w1, b1, q1_qw, q1_cw, q1_cb, out
                 if first > 0:
                     quantise_h1(h1_grouped, g - 1)
                 multiply_first(first, quantised, banks)
+                warm_up(FILL.get(2 * g + first // 2, 0))
             if g == SLICES - 1:
                 load_half()
 
@@ -452,6 +458,7 @@ def tile_quantumneuralnetwork_pa_kernel(tc, h0, w1, b1, q1_qw, q1_cw, q1_cb, out
                             start=(g == 0),
                             stop=(g == PASSES - 1),
                         )
+                warm_up(FILL.get(step, 0))
                 step += 1
             done = [
                 (is_turned, start // P + t if is_turned else (start, end, t), banks[t]) for t in range(tiles)

import math
from contextlib import ExitStack

import concourse.mybir as mybir
from concourse.masks import make_identity

F32 = mybir.dt.float32
BF16 = mybir.dt.bfloat16
U32 = mybir.dt.uint32
U8 = mybir.dt.uint8
FP8X4 = mybir.dt.float8_e4m3fn_x4
ACT = mybir.ActivationFunctionType
ALU = mybir.AluOpType

P = 128
PACK = 4
K_PASS = P * PACK
B = 512
H = 2048
DEPTH = 3
SIN, COS = 0, 1
THETA, PHI = 0, 1
PASSES = H // K_PASS
B_TILES = B // P
H_TILES = H // P
SLICE = 512
GROUPS = H // SLICE
HALF = 1024
SLICES = HALF // SLICE
HALVES = H // HALF
RUN = 4
HEAD_VECTOR_COLS = 336
VECTOR_COLS_1 = 48
VECTOR_COLS_TURNED = 256
VECTOR_COLS_ROWS = 0
HALVES_IN_SBUF = 3

ANGLES = DEPTH * H_TILES
FILLED_ROWS = ANGLES + H_TILES
ROUND_MAGIC = 1.5 * 2.0**23
PI_SAFE = 3.1415925

GROUPS_2 = [(0, 512, True), (512, 1024, False), (1024, 1536, True), (1536, 1792, False), (1792, 2048, False)]
BIAS_ROWS = [512, 1536]

FILL = {1: 2, 2: 2, 3: 2, 4: 2, 5: 2, 6: 2, 7: 2, 9: 6}

FLOPS = 2 * (2 * B * H * H)


def by_runs(rows):
    return rows.rearrange("p t (c i) -> p c t i", i=RUN)


def by_words(grouped):
    return grouped.rearrange("p (c i) t -> p c t i", i=RUN)


def regroup(nc, rows, grouped, vector_cols):
    vector_share = slice(0, vector_cols)
    scalar_share = slice(vector_cols, rows.shape[2])
    if vector_cols > 0:
        nc.vector.tensor_copy(
            out=by_words(grouped[:, vector_share, :]), in_=by_runs(rows[:, :, vector_share])
        )
    if vector_cols < rows.shape[2]:
        nc.scalar.copy(out=by_words(grouped[:, scalar_share, :]), in_=by_runs(rows[:, :, scalar_share]))


def quantise(nc, grouped, codes, scales):
    nc.vector.quantize_mx(out=codes.bitcast(FP8X4), scales=scales, in_=grouped)


def tile_quantumneuralnetwork_pa_kernel(tc, h0, w1, b1, q1_qw, q1_cw, q1_cb, out):
    nc = tc.nc
    with ExitStack() as ctx:
        ctx.enter_context(tc.manual_schedule())
        keep = ctx.enter_context(tc.tile_pool(name="keep", bufs=1))
        raw_pool = ctx.enter_context(tc.tile_pool(name="raw", bufs=HALVES_IN_SBUF * PASSES))
        grouped_pool = ctx.enter_context(tc.tile_pool(name="grouped", bufs=4))
        weight_pool = ctx.enter_context(tc.tile_pool(name="weight", bufs=4))
        h1_pool = ctx.enter_context(tc.tile_pool(name="h1", bufs=2))
        tanh_pool = ctx.enter_context(tc.tile_pool(name="tanh", bufs=7))
        out_pool = ctx.enter_context(tc.tile_pool(name="out", bufs=3))
        psum = ctx.enter_context(tc.psum_pool(name="psum", bufs=6))
        turn_psum = ctx.enter_context(tc.psum_pool(name="turn_psum", bufs=2))

        qw_rows = keep.tile([ANGLES, P, PACK], BF16)
        small_rows = keep.tile([P, 2, P], BF16)
        nc.sync.dma_start(out=qw_rows[:], in_=q1_qw.rearrange("d (m q) a b -> (d m) q (a b)", q=P))
        nc.sync.dma_start(
            out=small_rows[ANGLES:FILLED_ROWS, 0, :], in_=b1.rearrange("(m q) -> m q", q=P)
        )
        nc.sync.dma_start(
            out=small_rows[ANGLES:FILLED_ROWS, 1, :], in_=q1_cb.rearrange("(m q) -> m q", q=P)
        )
        h0_sb = keep.tile([P, B_TILES, H], BF16)

        def load_h0(bt):
            nc.sync.dma_start(out=h0_sb[:, bt, :], in_=h0[bt * P : (bt + 1) * P, :])

        def chunk_view(half, c, cols):
            if half < HALVES:
                rows = w1[c * K_PASS : (c + 1) * K_PASS, half * HALF : (half + 1) * HALF]
                return rows.rearrange("(u p e) n -> u p e n", u=2, e=2)[:, :, :, cols]
            rows = q1_cw[c * K_PASS : (c + 1) * K_PASS, (half - HALVES) * HALF : (half - HALVES + 1) * HALF]
            return rows.rearrange("(t p) n -> p t n", p=P)[:, :, cols]

        halves = []

        def weight_rows(half, c, start, width):
            return halves[half][c][:, start // SLICE, :, start % SLICE : start % SLICE + width]

        def new_half():
            halves.append(
                [raw_pool.tile([P, SLICES, PACK, SLICE], BF16, tag="raw", name="raw%d" % c) for c in range(PASSES)]
            )

        def load_slice(c, i):
            cols = slice(i * SLICE, (i + 1) * SLICE)
            view = chunk_view(len(halves) - 1, c, cols)
            tile = halves[-1][c][:, i]
            if len(halves) <= HALVES:
                for u in range(2):
                    nc.sync.dma_start(out=tile[:, 2 * u : 2 * u + 2, :], in_=view[u])
            else:
                nc.sync.dma_start(out=tile, in_=view)

        def load_half():
            new_half()
            for i in range(SLICES):
                for c in range(PASSES):
                    load_slice(c, i)

        new_half()
        for pair in range(PASSES // 2):
            for c in (2 * pair, 2 * pair + 1):
                load_slice(c, 0)
            for bt in (2 * pair, 2 * pair + 1):
                load_h0(bt)
        for c in range(PASSES):
            load_slice(c, 1)
        for i in range(1, HALVES_IN_SBUF):
            load_half()

        ident_f32 = keep.tile([P, P], F32)
        make_identity(nc, ident_f32[:])
        ident_bf16 = keep.tile([P, P], BF16)
        nc.vector.tensor_copy(out=ident_bf16[:], in_=ident_f32[:])

        angle_factor = keep.tile([P, 2, 1], F32)
        nc.vector.memset(angle_factor[:, 0, :], 2.0)
        nc.vector.memset(angle_factor[:, 1, :], 1.0)
        warm = keep.tile([P, 1], F32)
        nc.scalar.activation(out=warm[:], in_=angle_factor[:, 1, :], func=ACT.Sin)

        nc.gpsimd.memset(small_rows[FILLED_ROWS:P], 0.0)
        nc.vector.tensor_copy(
            out=small_rows[0:ANGLES], in_=qw_rows[:].rearrange("r q e -> r e q")[:, 0:PACK:3, :]
        )
        small_cols = psum.tile([P, 2, P], BF16, tag="bank")
        for h in range(2):
            nc.tensor.transpose(small_cols[:, h, :], small_rows[:, h, :], ident_bf16[:])

        zeros = keep.tile([P, SLICE], BF16)
        nc.gpsimd.memset(zeros[:], 0.0)

        def warm_up(products):
            if products == 0:
                return
            bank = turn_psum.tile([P, SLICE], F32, tag="turned", name="warm_bank")
            for i in range(products):
                nc.tensor.matmul(out=bank[:], lhsT=ident_bf16[:], rhs=zeros[:], start=True, stop=True)

        warm_up(8)
        args = keep.tile([P, 2, 2, ANGLES], F32)
        nc.vector.tensor_mul(
            out=args[:, 0],
            in0=small_cols[:, :, 0:ANGLES],
            in1=angle_factor[:].to_broadcast([P, 2, ANGLES]),
        )
        nc.vector.tensor_scalar_add(out=args[:, 1], in0=args[:, 0], scalar1=math.pi / 2.0)
        args_flat = args[:].rearrange("p f h r -> p (f h r)")
        turns = keep.tile([P, 2 * 2 * ANGLES], F32)
        nc.vector.tensor_scalar(
            out=turns[:], in0=args_flat, scalar1=1.0 / (2.0 * math.pi), scalar2=ROUND_MAGIC,
            op0=ALU.mult, op1=ALU.add,
        )
        nc.vector.tensor_scalar_sub(out=turns[:], in0=turns[:], scalar1=ROUND_MAGIC)
        nc.vector.scalar_tensor_tensor(
            out=args_flat, in0=turns[:], scalar=-2.0 * math.pi, in1=args_flat,
            op0=ALU.mult, op1=ALU.add,
        )
        nc.vector.tensor_scalar(
            out=args_flat, in0=args_flat, scalar1=-PI_SAFE, scalar2=PI_SAFE,
            op0=ALU.max, op1=ALU.min,
        )
        def quantise_pair(grouped, codes, scales, first):
            quantise(
                nc,
                grouped[:].rearrange("p j c t -> p (j c t)"),
                codes[:, first : first + 2, :].rearrange("p j c -> p (j c)"),
                scales[:, first : first + 2, :].rearrange("p j c -> p (j c)"),
            )

        steps = [
            (g * SLICE // HALF, g * SLICE % HALF, SLICE, first)
            for g in range(GROUPS)
            for first in range(0, PASSES, 2)
        ]
        for start, end, is_turned in GROUPS_2:
            for first in range(0, PASSES, 2):
                steps.append((HALVES + start // HALF, start % HALF, end - start, first))

        def regroup_pass(step, j, grouped, vector_cols):
            half, start, width, first = steps[step]
            regroup(nc, weight_rows(half, first + j, start, width), grouped[:, j], vector_cols)

        def new_grouped(width):
            return grouped_pool.tile([P, 2, width, PACK], BF16, align_bytes=64, tag="grouped", name="grouped")

        def regroup_step(step, vector_cols):
            width = steps[step][2]
            grouped = new_grouped(width)
            regroup_pass(step, 0, grouped, width)
            regroup_pass(step, 1, grouped, min(vector_cols, width))
            return grouped

        h0_words = h0_sb[:].bitcast(F32)
        words_in_pass = K_PASS // 2
        h0_codes = keep.tile([P, PASSES, B], U32, align_bytes=64)
        h0_scales = keep.tile([P, PASSES, B], U8, align_bytes=64)

        def transpose_h0(pair):
            for c in range(PASSES):
                bank = psum.tile([P, 2, 2, P], F32, tag="bank", name="h0_bank%d" % c)
                for u in range(2):
                    for i in range(2):
                        nc.tensor.transpose(
                            bank[:, u, i, :],
                            h0_words[:, 2 * pair + i, c * words_in_pass + u * P : c * words_in_pass + (u + 1) * P],
                            ident_f32[:],
                        )
                copy = nc.scalar.copy if c % 2 == 0 else nc.vector.tensor_copy
                copy(
                    out=h0_grouped[c // 2][:, c % 2].bitcast(F32)[:, 2 * pair * P : 2 * (pair + 1) * P, :],
                    in_=bank[:].rearrange("p u i b -> p (i b) u"),
                )

        def quantise_step(grouped, width):
            codes = weight_pool.tile([P, 2, width], U32, align_bytes=64, tag="codes", name="codes")
            scales = weight_pool.tile([P, 2, width], U8, align_bytes=64, tag="scales", name="scales")
            quantise_pair(grouped, codes, scales, 0)
            return codes, scales

        grouped = new_grouped(SLICE)
        h0_grouped = [
            grouped_pool.tile([P, 2, B, PACK], BF16, align_bytes=64, tag="grouped", name="h0_grouped%d" % i)
            for i in range(PASSES // 2)
        ]
        regroup_pass(0, 0, grouped, HEAD_VECTOR_COLS)
        sincos = keep.tile([P, 2, 2, DEPTH, H_TILES], F32)
        nc.scalar.activation(
            out=sincos[:].rearrange("p f h d m -> p (f h d m)"), in_=args_flat, func=ACT.Sin
        )
        nc.scalar.activation(out=warm[:], in_=angle_factor[:, 1, :], func=ACT.Tanh)
        regroup_pass(0, 1, grouped, SLICE)
        biases = keep.tile([P, 2, H_TILES], F32)
        nc.vector.tensor_copy(out=biases[:], in_=small_cols[:, :, ANGLES:FILLED_ROWS])

        def twice(table):
            return table.unsqueeze(1).to_broadcast([P, 2, H_TILES])

        z0 = sincos[:, COS, THETA, 0, :]
        yx0 = keep.tile([P, 2, H_TILES], F32)
        nc.gpsimd.tensor_mul(out=yx0[:], in0=sincos[:, :, PHI, 0, :], in1=twice(sincos[:, SIN, THETA, 0, :]))
        by_z0 = keep.tile([P, 2, H_TILES], F32)
        by_x0 = keep.tile([P, 2, H_TILES], F32)
        nc.gpsimd.tensor_mul(out=by_z0[:], in0=sincos[:, :, THETA, 1, :], in1=twice(z0))
        nc.gpsimd.tensor_mul(out=by_x0[:], in0=sincos[:, :, THETA, 1, :], in1=twice(yx0[:, 1, :]))
        y_part = keep.tile([P, H_TILES], F32)
        nc.gpsimd.tensor_mul(out=y_part[:], in0=yx0[:, 0, :], in1=sincos[:, SIN, PHI, 1, :])
        xz1 = keep.tile([P, 2, H_TILES], F32)
        nc.gpsimd.tensor_sub(out=xz1[:, 1, :], in0=by_z0[:, COS, :], in1=by_x0[:, SIN, :])
        x_part = keep.tile([P, H_TILES], F32)
        nc.gpsimd.tensor_add(out=x_part[:], in0=by_z0[:, SIN, :], in1=by_x0[:, COS, :])
        nc.gpsimd.tensor_mul(out=x_part[:], in0=x_part[:], in1=sincos[:, COS, PHI, 1, :])
        nc.gpsimd.tensor_sub(out=xz1[:, 0, :], in0=x_part[:], in1=y_part[:])
        by_xz1 = keep.tile([P, 2, H_TILES], F32)
        nc.gpsimd.tensor_mul(out=by_xz1[:], in0=sincos[:, :, THETA, 2, :], in1=xz1[:])
        out_bias = keep.tile([P, H_TILES], F32)
        nc.gpsimd.tensor_sub(out=out_bias[:], in0=by_xz1[:, COS, :], in1=by_xz1[:, SIN, :])
        nc.gpsimd.tensor_scalar(
            out=out_bias[:], in0=out_bias[:], scalar1=1.0, scalar2=0.5, op0=ALU.add, op1=ALU.mult
        )
        nc.gpsimd.tensor_add(out=out_bias[:], in0=out_bias[:], in1=biases[:, 1, :])

        quantised = [quantise_step(grouped, SLICE)]
        transpose_h0(0)
        warm_up(6)
        quantised.append(quantise_step(regroup_step(1, VECTOR_COLS_1), SLICE))
        transpose_h0(1)
        warm_up(2)
        for first in range(0, PASSES, 2):
            quantise_pair(h0_grouped[first // 2], h0_codes, h0_scales, first)
        ahead = regroup_step(2, VECTOR_COLS_1)

        h1_codes = keep.tile([P, PASSES, B], U32, align_bytes=64)
        h1_scales = keep.tile([P, PASSES, B], U8, align_bytes=64)

        def relu(h1_rows, g, t, bank):
            m = g * PACK + t
            nc.scalar.activation(
                out=h1_rows[:, t, :], in_=bank[:], func=ACT.Relu, bias=biases[:, 0, m : m + 1]
            )

        def regroup_h1(h1_rows):
            grouped = h1_pool.tile([P, B, PACK], BF16, align_bytes=64, tag="h1_grouped", name="h1_grouped")
            nc.vector.tensor_copy(out=by_words(grouped[:]), in_=by_runs(h1_rows[:]))
            return grouped

        def quantise_h1(grouped, g):
            quantise(nc, grouped[:].rearrange("p b t -> p (b t)"), h1_codes[:, g, :], h1_scales[:, g, :])

        out_tiles = out.rearrange("(i b) u -> b i u", b=P)

        out_bias_rows = keep.tile([P, len(BIAS_ROWS), SLICE], F32)

        def spread_out_bias(n):
            bank = turn_psum.tile([P, B_TILES, P], F32, tag="turned", name="bias_bank")
            for i in range(SLICE // P):
                m = BIAS_ROWS[n] // P + i
                nc.tensor.transpose(bank[:, i, :], out_bias[:, m : m + 1].to_broadcast([P, P]), ident_f32[:])
            nc.scalar.copy(
                out=out_bias_rows[:, n, :], in_=bank[:].rearrange("p i q -> p (i q)")
            )

        def finish_rows(start, end, bt, bank):
            result = tanh_pool.tile([P, end - start], F32, tag="result", name="result")
            n = BIAS_ROWS.index(start // SLICE * SLICE)
            bias = out_bias_rows[:, n, start % SLICE : start % SLICE + end - start]
            nc.vector.tensor_add(out=result[:], in0=bank[:], in1=bias)
            nc.scalar.activation(out=result[:], in_=result[:], func=ACT.Tanh)
            nc.sync.dma_start(out=out[bt * P : (bt + 1) * P, start:end], in_=result[:])

        def finish(m, bank):
            result = tanh_pool.tile([P, B], F32, tag="result", name="result")
            nc.scalar.activation(out=result[:], in_=bank[:], func=ACT.Tanh, bias=out_bias[:, m : m + 1])
            return result

        def turn(result):
            turned = turn_psum.tile([P, B_TILES, P], F32, tag="turned", name="turned")
            for bt in range(B_TILES):
                nc.tensor.transpose(turned[:, bt, :], result[:, bt * P : (bt + 1) * P], ident_f32[:])
            return turned

        def store(m, turned, copy):
            rows = out_pool.tile([P, B_TILES, len(turned) * P], F32, tag="rows", name="rows")
            for i in range(len(turned)):
                copy(out=rows[:, :, i * P : (i + 1) * P], in_=turned[i][:])
            nc.sync.dma_start(out=out_tiles[:, :, m * P : (m + len(turned)) * P], in_=rows[:])

        def multiply_first(first, quantised, banks):
            codes, scales = quantised
            for t in range(PACK):
                units = slice(t * P, (t + 1) * P)
                for c in (first, first + 1):
                    nc.tensor.matmul_mx(
                        out=banks[t][:],
                        lhsT=codes[:, c - first, units].bitcast(FP8X4),
                        lhsT_scale=scales[:, c - first, units],
                        rhs=h0_codes[:, c, :].bitcast(FP8X4),
                        rhs_scale=h0_scales[:, c, :],
                        start=(c == 0),
                        stop=(c == PASSES - 1),
                    )

        banks = [psum.tile([P, B], F32, tag="bank", name="h1_bank%d" % t) for t in range(PACK)]
        for first in range(0, PASSES, 2):
            multiply_first(first, quantised[first // 2], banks)
            warm_up(FILL.get(first // 2, 0))
        for g in range(1, GROUPS):
            last_banks = banks
            banks = [psum.tile([P, B], F32, tag="bank", name="h1_bank%d" % t) for t in range(PACK)]
            h1_rows = h1_pool.tile([P, PACK, B], BF16, tag="h1_rows")
            for first in range(0, PASSES, 2):
                grouped = ahead
                ahead = regroup_step(2 * g + first // 2 + 1, VECTOR_COLS_1)
                if first == 0:
                    for t in range(PACK):
                        relu(h1_rows, g - 1, t, last_banks[t])
                else:
                    h1_grouped = regroup_h1(h1_rows)
                    if g > 1:
                        for n in range(g - 2, len(BIAS_ROWS), 2):
                            spread_out_bias(n)
                quantised = quantise_step(grouped, SLICE)
                if first > 0:
                    quantise_h1(h1_grouped, g - 1)
                multiply_first(first, quantised, banks)
                warm_up(FILL.get(2 * g + first // 2, 0))
            if g == SLICES - 1:
                load_half()

        step = 2 * GROUPS
        done = []
        turned = []
        turned_m = 0
        h1_rows = h1_pool.tile([P, PACK, B], BF16, tag="h1_rows")
        for start, end, is_turned in GROUPS_2:
            width = end - start
            tiles = width // P if is_turned else B_TILES
            tile_cols = B if is_turned else width
            last_banks = banks
            banks = [psum.tile([P, tile_cols], F32, tag="bank", name="out_bank%d" % t) for t in range(tiles)]
            for first in range(0, PASSES, 2):
                grouped = ahead
                if start == 0 and first == 0:
                    for t in range(PACK):
                        relu(h1_rows, GROUPS - 1, t, last_banks[t])
                if start == 0 and first > 0:
                    h1_grouped = regroup_h1(h1_rows)
                    codes, scales = quantise_step(grouped, width)
                    quantise_h1(h1_grouped, GROUPS - 1)
                vector_cols = VECTOR_COLS_1 if start == 0 else VECTOR_COLS_TURNED if done[0][0] else VECTOR_COLS_ROWS
                if step + 1 < len(steps):
                    ahead = regroup_step(step + 1, vector_cols)
                part = done[0 : len(done) // 2] if first == 0 else done[len(done) // 2 :]
                results = []
                for kind, where, bank in part:
                    if kind:
                        results.append(finish(where, bank))
                    else:
                        finish_rows(where[0], where[1], where[2], bank)
                if turned:
                    store(turned_m, turned, nc.scalar.copy)
                    turned = []
                if start > 0 or first == 0:
                    codes, scales = quantise_step(grouped, width)
                for t in range(tiles):
                    if t == tiles // 2 and results:
                        turned = [turn(result) for result in results]
                        turned_m = part[0][1]
                    part_of_tile = slice(t * P, (t + 1) * P)
                    for g in (first, first + 1):
                        if is_turned:
                            lhs, lhs_scales = codes[:, g - first, part_of_tile], scales[:, g - first, part_of_tile]
                            rhs, rhs_scales = h1_codes[:, g, :], h1_scales[:, g, :]
                        else:
                            lhs, lhs_scales = h1_codes[:, g, part_of_tile], h1_scales[:, g, part_of_tile]
                            rhs, rhs_scales = codes[:, g - first, :], scales[:, g - first, :]
                        nc.tensor.matmul_mx(
                            out=banks[t][:],
                            lhsT=lhs.bitcast(FP8X4),
                            lhsT_scale=lhs_scales,
                            rhs=rhs.bitcast(FP8X4),
                            rhs_scale=rhs_scales,
                            start=(g == 0),
                            stop=(g == PASSES - 1),
                        )
                warm_up(FILL.get(step, 0))
                step += 1
            done = [
                (is_turned, start // P + t if is_turned else (start, end, t), banks[t]) for t in range(tiles)
            ]
        if turned:
            store(turned_m, turned, nc.vector.tensor_copy)
        for kind, where, bank in done:
            finish_rows(where[0], where[1], where[2], bank)
